import numpy as np
import ml_dtypes


def mxq(x, axis, fmt="e4m3"):
    dtype, down = {"e4m3": (ml_dtypes.float8_e4m3fn, 7), "e5m2": (ml_dtypes.float8_e5m2, 14)}[fmt]
    v = np.moveaxis(np.asarray(x, np.float32).astype(ml_dtypes.bfloat16).astype(np.float64), axis, -1)
    blocks = v.reshape(v.shape[:-1] + (-1, 32))
    amax = np.abs(blocks).max(-1, keepdims=True)
    byte = np.maximum(np.where(amax > 0, np.frexp(amax)[1] - 1 + 127, 0) - down, 1)
    scale = np.exp2(byte - 127.0)
    codes = (blocks / scale).astype(np.float32).astype(dtype).astype(np.float64)
    return np.moveaxis((codes * scale).reshape(v.shape), -1, axis)


WIDE = False


def mx_kscale(k):
    if not WIDE:
        return np.ones(k)
    levels = np.array([10, -10, 5, -5, 0])
    a = np.random.permutation(np.resize(levels, k // 512 * 4)).reshape(k // 512, 4)
    idx = np.arange(k)
    return np.exp2(a[idx // 512, idx % 128 // 32])


BF16 = ml_dtypes.bfloat16


def bf(x):
    return np.asarray(x, np.float32).astype(BF16)


def f64(x):
    return np.asarray(x).astype(np.float64)


B, N, HD, ED, F = 1, 32, 256, 512, 1024
TD = HD + HD
MD = TD + ED
EPS = 1e-5


def layer_norm(x, g, b):
    mu = x.mean(-1, keepdims=True)
    var = x.var(-1, keepdims=True)
    return (x - mu) * (1.0 / np.sqrt(var + EPS)) * g + b


def setup_inputs():
    s = mx_kscale(MD)
    sx, se = s[:HD], s[TD:]
    sr = np.concatenate([sx, sx, se])
    return {"p": bf(np.random.standard_normal((B, N, N, ED)) + 0.5 * np.random.standard_normal((B, N, N))[..., None]),
            "x_down": bf(np.random.standard_normal((B, N, HD)) * sx),
            "ln_edge_g": bf((1.0 + 0.1 * np.random.standard_normal(ED)) * se),
            "ln_edge_b": bf(0.1 * np.random.standard_normal(ED) * se),
            "W1": bf(np.random.standard_normal((MD, F)) / np.sqrt(MD) / sr[:, None]),
            "b1": bf(0.1 * np.random.standard_normal(F))}


def reference(p, x_down, ln_edge_g, ln_edge_b, W1, b1):
    p_ln = layer_norm(f64(p), f64(ln_edge_g), f64(ln_edge_b))
    xd = f64(x_down)
    edge_bias = np.concatenate([np.broadcast_to(xd[:, :, None, :], (B, N, N, HD)),
                                np.broadcast_to(xd[:, None, :, :], (B, N, N, HD))], axis=-1)
    z_in = np.concatenate([edge_bias, p_ln], axis=-1)
    return np.maximum((mxq(z_in, 3, "e4m3") @ mxq(f64(W1), 0, "e4m3")) + f64(b1), 0.0)

@@ -1,0 +1,245 @@
+from contextlib import ExitStack
+
+import concourse.mybir as mybir
+from concourse.masks import make_identity
+
+F32 = mybir.dt.float32
+BF16 = mybir.dt.bfloat16
+I32 = mybir.dt.int32
+U32 = mybir.dt.uint32
+U8 = mybir.dt.uint8
+FP8X4 = mybir.dt.float8_e4m3fn_x4
+ALU = mybir.AluOpType
+ACT = mybir.ActivationFunctionType
+
+P = 128
+NODES = 32
+HD = 256
+ED = 512
+F = 1024
+MT = 8
+NH = 512
+EPS = 1e-5
+FLOPS = 2 * 1024 * 1024 * 1024
+
+A_ENG = {(0, 0): "g", (1, 0): "s", (0, 1): "g", (1, 1): "s"}
+D_ENG = ["g", "s", "g", "s", "g", "s", "g", "s"]
+H_ENG = ["s", "g", "s", "g", "s", "g", "s", "g"]
+
+
+def regroup(nc, eng, dst, src):
+    dv = dst.rearrange("p (c i) t -> p c t i", i=4)
+    sv = src.rearrange("p t (c i) -> p c t i", i=4)
+    if eng == "v":
+        nc.vector.tensor_copy(out=dv, in_=sv)
+    elif eng == "s":
+        nc.scalar.copy(out=dv, in_=sv)
+    else:
+        nc.gpsimd.tensor_scalar(out=dv, in0=sv, scalar1=1.0, scalar2=0.0, op0=ALU.mult, op1=ALU.add)
+
+
+def tile_edgeupdaterwrapper_v01_pa_kernel(tc, p, x_down, ln_edge_g, ln_edge_b, W1, b1, out):
+    nc = tc.nc
+    p_v = p.rearrange("b i (a m) k -> (b i a) m k", m=MT)
+    out_v = out.rearrange("b i (a m) f -> (b i a) m f", m=MT)
+
+    with ExitStack() as ctx:
+        const = ctx.enter_context(tc.tile_pool(name="const", bufs=1))
+        work = ctx.enter_context(tc.tile_pool(name="work", bufs=1))
+        ps_tp = ctx.enter_context(tc.psum_pool(name="ps_tp", bufs=1))
+        ps_acc = ctx.enter_context(tc.psum_pool(name="ps_acc", bufs=4))
+
+        p_sb = const.tile([P, MT, ED], BF16, name="p_sb")
+        wraw = {}
+        for c in range(2):
+            for n in range(2):
+                wraw[(c, n)] = const.tile([P, 4, NH], BF16, name="wraw%d%d" % (c, n))
+
+        def load_w(c, n):
+            cols = slice(n * NH, (n + 1) * NH)
+            if c == 0:
+                src = W1[0:512, cols].rearrange("(q j) w -> q j w", j=4)
+            else:
+                src = W1[512:1024, cols].rearrange("(t q) w -> q t w", q=P)
+            nc.sync.dma_start(out=wraw[(c, n)][:], in_=src)
+
+        nc.sync.dma_start(out=p_sb[:, 0:4, :], in_=p_v[:, 0:4, :])
+        load_w(0, 0)
+        nc.sync.dma_start(out=p_sb[:, 4:8, :], in_=p_v[:, 4:8, :])
+        load_w(1, 0)
+        load_w(0, 1)
+        load_w(1, 1)
+
+        eps_t = const.tile([P, 1], F32, name="eps_t")
+        nc.vector.memset(eps_t[:], EPS)
+        junk = const.tile([P, 1], F32, name="junk")
+        nc.scalar.activation(out=junk[:], in_=eps_t[:], func=ACT.Sqrt)
+
+        xx = const.tile([P, 3 * HD], BF16, name="xx")
+        nc.vector.memset(xx[:], 0.0)
+        su = const.tile([P, P], BF16, name="su")
+        nc.vector.memset(su[:], 0.0)
+        bz = const.tile([P, F], BF16, name="bz")
+        nc.vector.memset(bz[:], 0.0)
+        ones_b = const.tile([P, P], BF16, name="ones_b")
+        nc.vector.memset(ones_b[:], 1.0)
+        nc.scalar.dma_start(out=xx[0:NODES, HD : 2 * HD], in_=x_down.rearrange("b n k -> (b n) k"))
+        nc.scalar.dma_start(out=su[0:4, :], in_=ln_edge_g.rearrange("(t q) -> t q", q=P))
+        nc.scalar.dma_start(out=su[4:8, :], in_=ln_edge_b.rearrange("(t q) -> t q", q=P))
+        nc.scalar.dma_start(out=bz[0:1, :], in_=b1.rearrange("(o f) -> o f", o=1))
+
+        ident_f = const.tile([P, P], F32, name="ident_f")
+        make_identity(nc, ident_f[:])
+        ident_b = const.tile([P, P], BF16, name="ident_b")
+        nc.vector.tensor_copy(out=ident_b[:], in_=ident_f[:])
+        sel_i = const.tile([P, P], BF16, name="sel_i")
+        nc.vector.tensor_copy(
+            out=sel_i[:].rearrange("p (i a) -> p i a", a=4),
+            in_=ident_b[:, 0:NODES].unsqueeze(2).to_broadcast([P, NODES, 4]),
+        )
+        sel_j = const.tile([P, P], BF16, name="sel_j")
+        nc.vector.tensor_copy(
+            out=sel_j[:].rearrange("p (r m a) -> p r m a", r=4, a=4),
+            in_=ident_b[:, 0:NODES].rearrange("p (a m) -> p m a", a=4).unsqueeze(1).to_broadcast([P, 4, MT, 4]),
+        )
+        xs = const.tile([P, P], U8, name="xs", align_bytes=64)
+        nc.vector.memset(xs[:].bitcast(I32), 0)
+
+        su_ps = ps_acc.tile([P, P], BF16, name="su_ps", tag="acc")
+        nc.tensor.transpose(su_ps[:], su[:], ident_b[:])
+        gb = const.tile([P, 8], F32, name="gb")
+        nc.scalar.copy(out=gb[:], in_=su_ps[:, 0:8])
+
+        xp = ps_acc.tile([P, 4, P], F32, name="xp", tag="acc")
+        for t in range(4):
+            nc.tensor.matmul(xp[:, t, :], lhsT=xx[:, HD + t : 3 * HD : 4], rhs=sel_i[:], start=True, stop=False)
+            nc.tensor.matmul(xp[:, t, :], lhsT=xx[:, t : 2 * HD : 4], rhs=sel_j[:], start=False, stop=True)
+        xg = const.tile([P, P, 4], BF16, name="xg", align_bytes=64)
+        nc.scalar.copy(out=xg[:], in_=xp[:].rearrange("p t c -> p c t"))
+        xc = const.tile([P, P], U32, name="xc", align_bytes=64)
+        nc.vector.quantize_mx(out=xc[:].bitcast(FP8X4), scales=xs[:], in_=xg[:].rearrange("p c t -> p (c t)"))
+        c0 = const.tile([P, MT * P], U32, name="c0", align_bytes=64)
+        s0 = const.tile([P, MT * P], U8, name="s0", align_bytes=64)
+        xc_i = xc[:].bitcast(I32)
+        xs_i = xs[:].bitcast(I32)
+        c0_i = c0[:].bitcast(I32)
+        s0_i = s0[:].bitcast(I32)
+        H = 64
+        nc.vector.tensor_copy(
+            out=c0_i[0:H, :].rearrange("p (m c) -> p m c", m=MT),
+            in_=xc_i[0:H, :].unsqueeze(1).to_broadcast([H, MT, P]),
+        )
+        nc.vector.tensor_copy(
+            out=c0_i[H:P, :].rearrange("p (m r a) -> p m r a", m=MT, a=4),
+            in_=xc_i[H:P, 0:32].rearrange("p (m a) -> p m a", a=4).unsqueeze(2).to_broadcast([H, MT, 32, 4]),
+        )
+        nc.vector.tensor_copy(
+            out=s0_i[0:H, :].rearrange("p (m c) -> p m c", m=MT),
+            in_=xs_i[0:H, :].unsqueeze(1).to_broadcast([H, MT, 32]),
+        )
+        nc.vector.tensor_copy(
+            out=s0_i[H:P, :].rearrange("p (m r) -> p m r", m=MT),
+            in_=xs_i[H:P, 0:MT].unsqueeze(2).to_broadcast([H, MT, 32]),
+        )
+
+        bias_sb = const.tile([P, F], F32, name="bias_sb")
+        for n in range(2):
+            b_ps = ps_acc.tile([P, NH], F32, name="b_ps", tag="acc")
+            nc.tensor.matmul(b_ps[:], lhsT=ones_b[:], rhs=bz[:, n * NH : (n + 1) * NH], start=True, stop=True)
+            nc.scalar.copy(out=bias_sb[:, n * NH : (n + 1) * NH], in_=b_ps[:])
+
+        stats = const.tile([P, MT, 6], F32, name="stats")
+        mv = const.tile([P, MT, 2], F32, name="mv")
+        std = const.tile([P, MT], F32, name="std")
+        rstd = const.tile([P, MT], F32, name="rstd")
+        nmr = const.tile([P, MT], F32, name="nmr")
+        zc = const.tile([P, MT * P], U32, name="zc", align_bytes=64)
+        zs = const.tile([P, MT * P], U8, name="zs", align_bytes=64)
+        wc = [const.tile([P, F], U32, name="wc%d" % c, align_bytes=64) for c in range(2)]
+        ws = [const.tile([P, F], U8, name="ws%d" % c, align_bytes=64) for c in range(2)]
+
+        def ln_stats(g):
+            ms = slice(4 * g, 4 * g + 4)
+            for m in range(4 * g, 4 * g + 4):
+                nc.vector.bn_stats(out=stats[:, m, :], in_=p_sb[:, m, :])
+                nc.vector.bn_aggr(out=mv[:, m, :], in_=stats[:, m, :])
+            nc.scalar.activation(out=std[:, ms], in_=mv[:, ms, 1], func=ACT.Sqrt, bias=eps_t[:, 0:1])
+            nc.vector.reciprocal(out=rstd[:, ms], in_=std[:, ms])
+            nc.vector.scalar_tensor_tensor(
+                out=nmr[:, ms], in0=mv[:, ms, 0], scalar=-1.0, in1=rstd[:, ms], op0=ALU.mult, op1=ALU.mult
+            )
+
+        def ln_apply(g):
+            tps = [ps_tp.tile([P, 4, P], F32, name="tp%d" % t) for t in range(4)]
+            for mi in range(4):
+                m = 4 * g + mi
+                xn = work.tile([P, ED], F32, name="xn%d" % m)
+                if D_ENG[m] == "s":
+                    nc.scalar.activation(
+                        out=xn[:], in_=p_sb[:, m, :], func=ACT.Identity, scale=rstd[:, m : m + 1], bias=nmr[:, m : m + 1]
+                    )
+                else:
+                    nc.gpsimd.tensor_scalar(
+                        out=xn[:], in0=p_sb[:, m, :], scalar1=rstd[:, m : m + 1], scalar2=nmr[:, m : m + 1],
+                        op0=ALU.mult, op1=ALU.add,
+                    )
+                for t in range(4):
+                    nc.tensor.transpose(tps[t][:, mi, :], xn[:, t * P : (t + 1) * P], ident_f[:])
+            zp = work.tile([P, 4, NH], BF16, name="zp%d" % g)
+            for t in range(4):
+                nc.scalar.activation(
+                    out=zp[:, t, :], in_=tps[t][:].rearrange("p m c -> p (m c)"), func=ACT.Identity,
+                    scale=gb[:, t : t + 1], bias=gb[:, 4 + t : 5 + t],
+                )
+            zg = work.tile([P, NH, 4], BF16, name="zg%d" % g, align_bytes=64)
+            regroup(nc, "v", zg[:], zp[:])
+            cols = slice(g * NH, (g + 1) * NH)
+            nc.vector.quantize_mx(out=zc[:, cols].bitcast(FP8X4), scales=zs[:, cols], in_=zg[:].rearrange("p w t -> p (w t)"))
+
+        def w_prep(c, n):
+            wg = work.tile([P, NH, 4], BF16, name="wg%d%d" % (c, n), align_bytes=64)
+            regroup(nc, A_ENG[(c, n)], wg[:], wraw[(c, n)][:])
+            cols = slice(n * NH, (n + 1) * NH)
+            nc.vector.quantize_mx(
+                out=wc[c][:, cols].bitcast(FP8X4), scales=ws[c][:, cols], in_=wg[:].rearrange("p w t -> p (w t)")
+            )
+
+        o_sb = [const.tile([P, F], F32, name="o%d" % m) for m in range(MT)]
+
+        def mm(m, n):
+            rows = slice(m * P, (m + 1) * P)
+            cols = slice(n * NH, (n + 1) * NH)
+            acc = ps_acc.tile([P, NH], F32, name="acc", tag="acc")
+            nc.tensor.matmul_mx(
+                out=acc[:], lhsT=c0[:, rows].bitcast(FP8X4), lhsT_scale=s0[:, rows],
+                rhs=wc[0][:, cols].bitcast(FP8X4), rhs_scale=ws[0][:, cols], start=True, stop=False,
+            )
+            nc.tensor.matmul_mx(
+                out=acc[:], lhsT=zc[:, rows].bitcast(FP8X4), lhsT_scale=zs[:, rows],
+                rhs=wc[1][:, cols].bitcast(FP8X4), rhs_scale=ws[1][:, cols], start=False, stop=True,
+            )
+            nc.vector.tensor_tensor(out=o_sb[m][:, cols], in0=acc[:], in1=bias_sb[:, cols], op=ALU.add)
+
+        def finish(m):
+            if H_ENG[m] == "s":
+                nc.scalar.activation(out=o_sb[m][:], in_=o_sb[m][:], func=ACT.Relu)
+            else:
+                nc.gpsimd.tensor_scalar(
+                    out=o_sb[m][:], in0=o_sb[m][:], scalar1=float("inf"), scalar2=0.0, op0=ALU.min, op1=ALU.max
+                )
+            nc.sync.dma_start(out=out_v[:, m, :], in_=o_sb[m][:])
+
+        ln_stats(0)
+        w_prep(0, 0)
+        ln_stats(1)
+        ln_apply(0)
+        w_prep(1, 0)
+        w_prep(0, 1)
+        ln_apply(1)
+        w_prep(1, 1)
+        for g in range(2):
+            for n in range(2):
+                for mi in range(4):
+                    mm(4 * g + mi, n)
+            for mi in range(4):
+                finish(4 * g + mi)

@@ -22,10 +22,6 @@ NH = 512
 EPS = 1e-5
 FLOPS = 2 * 1024 * 1024 * 1024
 
-A_ENG = {(0, 0): "g", (1, 0): "s", (0, 1): "g", (1, 1): "s"}
-D_ENG = ["g", "s", "g", "s", "g", "s", "g", "s"]
-H_ENG = ["s", "g", "s", "g", "s", "g", "s", "g"]
-
 
 def regroup(nc, eng, dst, src):
     dv = dst.rearrange("p (c i) t -> p c t i", i=4)
@@ -45,109 +41,32 @@ def tile_edgeupdaterwrapper_v01_pa_kernel(tc, p, x_down, ln_edge_g, ln_edge_b, W
 
     with ExitStack() as ctx:
         const = ctx.enter_context(tc.tile_pool(name="const", bufs=1))
-        work = ctx.enter_context(tc.tile_pool(name="work", bufs=1))
         ps_tp = ctx.enter_context(tc.psum_pool(name="ps_tp", bufs=1))
         ps_acc = ctx.enter_context(tc.psum_pool(name="ps_acc", bufs=4))
+        ctx.enter_context(tc.manual_schedule())
 
         p_sb = const.tile([P, MT, ED], BF16, name="p_sb")
         wraw = {}
+        wg = {}
         for c in range(2):
             for n in range(2):
                 wraw[(c, n)] = const.tile([P, 4, NH], BF16, name="wraw%d%d" % (c, n))
-
-        def load_w(c, n):
-            cols = slice(n * NH, (n + 1) * NH)
-            if c == 0:
-                src = W1[0:512, cols].rearrange("(q j) w -> q j w", j=4)
-            else:
-                src = W1[512:1024, cols].rearrange("(t q) w -> q t w", q=P)
-            nc.sync.dma_start(out=wraw[(c, n)][:], in_=src)
-
-        nc.sync.dma_start(out=p_sb[:, 0:4, :], in_=p_v[:, 0:4, :])
-        load_w(0, 0)
-        nc.sync.dma_start(out=p_sb[:, 4:8, :], in_=p_v[:, 4:8, :])
-        load_w(1, 0)
-        load_w(0, 1)
-        load_w(1, 1)
-
+                wg[(c, n)] = const.tile([P, NH, 4], BF16, name="wg%d%d" % (c, n), align_bytes=64)
         eps_t = const.tile([P, 1], F32, name="eps_t")
-        nc.vector.memset(eps_t[:], EPS)
         junk = const.tile([P, 1], F32, name="junk")
-        nc.scalar.activation(out=junk[:], in_=eps_t[:], func=ACT.Sqrt)
-
         xx = const.tile([P, 3 * HD], BF16, name="xx")
-        nc.vector.memset(xx[:], 0.0)
         su = const.tile([P, P], BF16, name="su")
-        nc.vector.memset(su[:], 0.0)
-        bz = const.tile([P, F], BF16, name="bz")
-        nc.vector.memset(bz[:], 0.0)
-        ones_b = const.tile([P, P], BF16, name="ones_b")
-        nc.vector.memset(ones_b[:], 1.0)
-        nc.scalar.dma_start(out=xx[0:NODES, HD : 2 * HD], in_=x_down.rearrange("b n k -> (b n) k"))
-        nc.scalar.dma_start(out=su[0:4, :], in_=ln_edge_g.rearrange("(t q) -> t q", q=P))
-        nc.scalar.dma_start(out=su[4:8, :], in_=ln_edge_b.rearrange("(t q) -> t q", q=P))
-        nc.scalar.dma_start(out=bz[0:1, :], in_=b1.rearrange("(o f) -> o f", o=1))
-
+        bias_bf = const.tile([P, F], BF16, name="bias_bf")
         ident_f = const.tile([P, P], F32, name="ident_f")
-        make_identity(nc, ident_f[:])
         ident_b = const.tile([P, P], BF16, name="ident_b")
-        nc.vector.tensor_copy(out=ident_b[:], in_=ident_f[:])
         sel_i = const.tile([P, P], BF16, name="sel_i")
-        nc.vector.tensor_copy(
-            out=sel_i[:].rearrange("p (i a) -> p i a", a=4),
-            in_=ident_b[:, 0:NODES].unsqueeze(2).to_broadcast([P, NODES, 4]),
-        )
         sel_j = const.tile([P, P], BF16, name="sel_j")
-        nc.vector.tensor_copy(
-            out=sel_j[:].rearrange("p (r m a) -> p r m a", r=4, a=4),
-            in_=ident_b[:, 0:NODES].rearrange("p (a m) -> p m a", a=4).unsqueeze(1).to_broadcast([P, 4, MT, 4]),
-        )
         xs = const.tile([P, P], U8, name="xs", align_bytes=64)
-        nc.vector.memset(xs[:].bitcast(I32), 0)
-
-        su_ps = ps_acc.tile([P, P], BF16, name="su_ps", tag="acc")
-        nc.tensor.transpose(su_ps[:], su[:], ident_b[:])
-        gb = const.tile([P, 8], F32, name="gb")
-        nc.scalar.copy(out=gb[:], in_=su_ps[:, 0:8])
-
-        xp = ps_acc.tile([P, 4, P], F32, name="xp", tag="acc")
-        for t in range(4):
-            nc.tensor.matmul(xp[:, t, :], lhsT=xx[:, HD + t : 3 * HD : 4], rhs=sel_i[:], start=True, stop=False)
-            nc.tensor.matmul(xp[:, t, :], lhsT=xx[:, t : 2 * HD : 4], rhs=sel_j[:], start=False, stop=True)
-        xg = const.tile([P, P, 4], BF16, name="xg", align_bytes=64)
-        nc.scalar.copy(out=xg[:], in_=xp[:].rearrange("p t c -> p c t"))
         xc = const.tile([P, P], U32, name="xc", align_bytes=64)
-        nc.vector.quantize_mx(out=xc[:].bitcast(FP8X4), scales=xs[:], in_=xg[:].rearrange("p c t -> p (c t)"))
+        xg = const.tile([P, P, 4], BF16, name="xg", align_bytes=64)
+        gb = const.tile([P, 8], F32, name="gb")
         c0 = const.tile([P, MT * P], U32, name="c0", align_bytes=64)
         s0 = const.tile([P, MT * P], U8, name="s0", align_bytes=64)
-        xc_i = xc[:].bitcast(I32)
-        xs_i = xs[:].bitcast(I32)
-        c0_i = c0[:].bitcast(I32)
-        s0_i = s0[:].bitcast(I32)
-        H = 64
-        nc.vector.tensor_copy(
-            out=c0_i[0:H, :].rearrange("p (m c) -> p m c", m=MT),
-            in_=xc_i[0:H, :].unsqueeze(1).to_broadcast([H, MT, P]),
-        )
-        nc.vector.tensor_copy(
-            out=c0_i[H:P, :].rearrange("p (m r a) -> p m r a", m=MT, a=4),
-            in_=xc_i[H:P, 0:32].rearrange("p (m a) -> p m a", a=4).unsqueeze(2).to_broadcast([H, MT, 32, 4]),
-        )
-        nc.vector.tensor_copy(
-            out=s0_i[0:H, :].rearrange("p (m c) -> p m c", m=MT),
-            in_=xs_i[0:H, :].unsqueeze(1).to_broadcast([H, MT, 32]),
-        )
-        nc.vector.tensor_copy(
-            out=s0_i[H:P, :].rearrange("p (m r) -> p m r", m=MT),
-            in_=xs_i[H:P, 0:MT].unsqueeze(2).to_broadcast([H, MT, 32]),
-        )
-
-        bias_sb = const.tile([P, F], F32, name="bias_sb")
-        for n in range(2):
-            b_ps = ps_acc.tile([P, NH], F32, name="b_ps", tag="acc")
-            nc.tensor.matmul(b_ps[:], lhsT=ones_b[:], rhs=bz[:, n * NH : (n + 1) * NH], start=True, stop=True)
-            nc.scalar.copy(out=bias_sb[:, n * NH : (n + 1) * NH], in_=b_ps[:])
-
         stats = const.tile([P, MT, 6], F32, name="stats")
         mv = const.tile([P, MT, 2], F32, name="mv")
         std = const.tile([P, MT], F32, name="std")
@@ -157,59 +76,143 @@ def tile_edgeupdaterwrapper_v01_pa_kernel(tc, p, x_down, ln_edge_g, ln_edge_b, W
         zs = const.tile([P, MT * P], U8, name="zs", align_bytes=64)
         wc = [const.tile([P, F], U32, name="wc%d" % c, align_bytes=64) for c in range(2)]
         ws = [const.tile([P, F], U8, name="ws%d" % c, align_bytes=64) for c in range(2)]
+        xn = [const.tile([P, ED], F32, name="xn%d" % m) for m in range(MT)]
+        zp = [const.tile([P, 4, NH], BF16, name="zp%d" % g) for g in range(2)]
+        zg = [const.tile([P, NH, 4], BF16, name="zg%d" % g, align_bytes=64) for g in range(2)]
+        o_sb = [const.tile([P, F], F32, name="o%d" % m) for m in range(MT)]
+
+        nc.vector.memset(su[:], 0.0)
+        nc.vector.memset(xx[:], 0.0)
+        nc.vector.memset(eps_t[:], EPS)
+        nc.vector.memset(xs[:].bitcast(I32), 0)
+        make_identity(nc, ident_f[:])
+        nc.scalar.activation(out=junk[:], in_=eps_t[:], func=ACT.Sqrt)
+
+        def load_w(c, n):
+            cols = slice(n * NH, (n + 1) * NH)
+            if c == 0:
+                src = W1[0:512, cols].rearrange("(q j) w -> q j w", j=4)
+            else:
+                src = W1[512:1024, cols].rearrange("(t q) w -> q t w", q=P)
+            nc.sync.dma_start(out=wraw[(c, n)][:], in_=src)
+
+        nc.sync.dma_start(out=p_sb[:, 0:2, :], in_=p_v[:, 0:2, :])
+        nc.sync.dma_start(out=xx[0:NODES, HD : 2 * HD], in_=x_down.rearrange("b n k -> (b n) k"))
+        nc.sync.dma_start(out=su[0:4, :], in_=ln_edge_g.rearrange("(t q) -> t q", q=P))
+        nc.sync.dma_start(out=su[4:8, :], in_=ln_edge_b.rearrange("(t q) -> t q", q=P))
+        load_w(0, 0)
+        nc.sync.dma_start(out=p_sb[:, 2:4, :], in_=p_v[:, 2:4, :])
+        load_w(1, 0)
+        nc.sync.dma_start(out=p_sb[:, 4:8, :], in_=p_v[:, 4:8, :])
+        load_w(0, 1)
+        load_w(1, 1)
+        nc.sync.dma_start(out=bias_bf[:], in_=b1.partition_broadcast(P))
+
+        nc.vector.tensor_copy(out=ident_b[:], in_=ident_f[:])
+        nc.vector.tensor_copy(
+            out=sel_i[:].rearrange("p (i a) -> p i a", a=4),
+            in_=ident_b[:, 0:NODES].unsqueeze(2).to_broadcast([P, NODES, 4]),
+        )
+        nc.vector.tensor_copy(
+            out=sel_j[:].rearrange("p (r m a) -> p r m a", r=4, a=4),
+            in_=ident_b[:, 0:NODES].rearrange("p (a m) -> p m a", a=4).unsqueeze(1).to_broadcast([P, 4, MT, 4]),
+        )
+
+        su_ps = ps_acc.tile([P, P], BF16, name="su_ps", tag="acc")
+        nc.tensor.transpose(su_ps[:], su[:], ident_b[:])
+        nc.scalar.copy(out=gb[:], in_=su_ps[:, 0:8])
+        xp = ps_acc.tile([P, 4, P], F32, name="xp", tag="acc")
+        for t in range(4):
+            nc.tensor.matmul(xp[:, t, :], lhsT=xx[:, HD + t : 3 * HD : 4], rhs=sel_i[:], start=True, stop=False)
+            nc.tensor.matmul(xp[:, t, :], lhsT=xx[:, t : 2 * HD : 4], rhs=sel_j[:], start=False, stop=True)
+        nc.scalar.copy(out=xg[:], in_=xp[:].rearrange("p t c -> p c t"))
+
+        def x_words():
+            nc.vector.quantize_mx(out=xc[:].bitcast(FP8X4), scales=xs[:], in_=xg[:].rearrange("p c t -> p (c t)"))
+            xc_i = xc[:].bitcast(I32)
+            xs_i = xs[:].bitcast(I32)
+            c0_i = c0[:].bitcast(I32)
+            s0_i = s0[:].bitcast(I32)
+            H = 64
+            nc.vector.tensor_copy(
+                out=c0_i[0:H, :].rearrange("p (m c) -> p m c", m=MT),
+                in_=xc_i[0:H, :].unsqueeze(1).to_broadcast([H, MT, P]),
+            )
+            nc.vector.tensor_copy(
+                out=c0_i[H:P, :].rearrange("p (m r a) -> p m r a", m=MT, a=4),
+                in_=xc_i[H:P, 0:32].rearrange("p (m a) -> p m a", a=4).unsqueeze(2).to_broadcast([H, MT, 32, 4]),
+            )
+            nc.vector.tensor_copy(
+                out=s0_i[0:H, :].rearrange("p (m c) -> p m c", m=MT),
+                in_=xs_i[0:H, :].unsqueeze(1).to_broadcast([H, MT, 32]),
+            )
+            nc.vector.tensor_copy(
+                out=s0_i[H:P, :].rearrange("p (m r) -> p m r", m=MT),
+                in_=xs_i[H:P, 0:MT].unsqueeze(2).to_broadcast([H, MT, 32]),
+            )
 
         def ln_stats(g):
-            ms = slice(4 * g, 4 * g + 4)
             for m in range(4 * g, 4 * g + 4):
                 nc.vector.bn_stats(out=stats[:, m, :], in_=p_sb[:, m, :])
                 nc.vector.bn_aggr(out=mv[:, m, :], in_=stats[:, m, :])
+
+        def ln_rstd(g):
+            ms = slice(4 * g, 4 * g + 4)
             nc.scalar.activation(out=std[:, ms], in_=mv[:, ms, 1], func=ACT.Sqrt, bias=eps_t[:, 0:1])
             nc.vector.reciprocal(out=rstd[:, ms], in_=std[:, ms])
             nc.vector.scalar_tensor_tensor(
                 out=nmr[:, ms], in0=mv[:, ms, 0], scalar=-1.0, in1=rstd[:, ms], op0=ALU.mult, op1=ALU.mult
             )
 
-        def ln_apply(g):
-            tps = [ps_tp.tile([P, 4, P], F32, name="tp%d" % t) for t in range(4)]
+        tps = {}
+
+        def ln_norm(g, eng):
+            for t in range(4):
+                tps[(g, t)] = ps_tp.tile([P, 4, P], F32, name="tp%d" % t)
             for mi in range(4):
                 m = 4 * g + mi
-                xn = work.tile([P, ED], F32, name="xn%d" % m)
-                if D_ENG[m] == "s":
+                if eng == "s":
                     nc.scalar.activation(
-                        out=xn[:], in_=p_sb[:, m, :], func=ACT.Identity, scale=rstd[:, m : m + 1], bias=nmr[:, m : m + 1]
+                        out=xn[m][:], in_=p_sb[:, m, :], func=ACT.Identity, scale=rstd[:, m : m + 1], bias=nmr[:, m : m + 1]
                     )
                 else:
                     nc.gpsimd.tensor_scalar(
-                        out=xn[:], in0=p_sb[:, m, :], scalar1=rstd[:, m : m + 1], scalar2=nmr[:, m : m + 1],
+                        out=xn[m][:], in0=p_sb[:, m, :], scalar1=rstd[:, m : m + 1], scalar2=nmr[:, m : m + 1],
                         op0=ALU.mult, op1=ALU.add,
                     )
                 for t in range(4):
-                    nc.tensor.transpose(tps[t][:, mi, :], xn[:, t * P : (t + 1) * P], ident_f[:])
-            zp = work.tile([P, 4, NH], BF16, name="zp%d" % g)
+                    nc.tensor.transpose(tps[(g, t)][:, mi, :], xn[m][:, t * P : (t + 1) * P], ident_f[:])
+
+        def ln_gain(g):
             for t in range(4):
                 nc.scalar.activation(
-                    out=zp[:, t, :], in_=tps[t][:].rearrange("p m c -> p (m c)"), func=ACT.Identity,
+                    out=zp[g][:, t, :], in_=tps[(g, t)][:].rearrange("p m c -> p (m c)"), func=ACT.Identity,
                     scale=gb[:, t : t + 1], bias=gb[:, 4 + t : 5 + t],
                 )
-            zg = work.tile([P, NH, 4], BF16, name="zg%d" % g, align_bytes=64)
-            regroup(nc, "v", zg[:], zp[:])
-            cols = slice(g * NH, (g + 1) * NH)
-            nc.vector.quantize_mx(out=zc[:, cols].bitcast(FP8X4), scales=zs[:, cols], in_=zg[:].rearrange("p w t -> p (w t)"))
 
-        def w_prep(c, n):
-            wg = work.tile([P, NH, 4], BF16, name="wg%d%d" % (c, n), align_bytes=64)
-            regroup(nc, A_ENG[(c, n)], wg[:], wraw[(c, n)][:])
-            cols = slice(n * NH, (n + 1) * NH)
+        def z_quant(g):
+            regroup(nc, "v", zg[g][:], zp[g][:])
+            cols = slice(g * NH, (g + 1) * NH)
             nc.vector.quantize_mx(
-                out=wc[c][:, cols].bitcast(FP8X4), scales=ws[c][:, cols], in_=wg[:].rearrange("p w t -> p (w t)")
+                out=zc[:, cols].bitcast(FP8X4), scales=zs[:, cols], in_=zg[g][:].rearrange("p w t -> p (w t)")
             )
 
-        o_sb = [const.tile([P, F], F32, name="o%d" % m) for m in range(MT)]
+        def w_regroup(c, n, eng):
+            regroup(nc, eng, wg[(c, n)][:], wraw[(c, n)][:])
+
+        def w_quant(c, n):
+            cols = slice(n * NH, (n + 1) * NH)
+            nc.vector.quantize_mx(
+                out=wc[c][:, cols].bitcast(FP8X4), scales=ws[c][:, cols], in_=wg[(c, n)][:].rearrange("p w t -> p (w t)")
+            )
+
+        accs = {}
 
         def mm(m, n):
             rows = slice(m * P, (m + 1) * P)
             cols = slice(n * NH, (n + 1) * NH)
             acc = ps_acc.tile([P, NH], F32, name="acc", tag="acc")
+            accs[(m, n)] = acc
             nc.tensor.matmul_mx(
                 out=acc[:], lhsT=c0[:, rows].bitcast(FP8X4), lhsT_scale=s0[:, rows],
                 rhs=wc[0][:, cols].bitcast(FP8X4), rhs_scale=ws[0][:, cols], start=True, stop=False,
@@ -218,28 +221,59 @@ def tile_edgeupdaterwrapper_v01_pa_kernel(tc, p, x_down, ln_edge_g, ln_edge_b, W
                 out=acc[:], lhsT=zc[:, rows].bitcast(FP8X4), lhsT_scale=zs[:, rows],
                 rhs=wc[1][:, cols].bitcast(FP8X4), rhs_scale=ws[1][:, cols], start=False, stop=True,
             )
-            nc.vector.tensor_tensor(out=o_sb[m][:, cols], in0=acc[:], in1=bias_sb[:, cols], op=ALU.add)
 
-        def finish(m):
-            if H_ENG[m] == "s":
-                nc.scalar.activation(out=o_sb[m][:], in_=o_sb[m][:], func=ACT.Relu)
+        def add_bias(m, n):
+            cols = slice(n * NH, (n + 1) * NH)
+            nc.vector.tensor_tensor(out=o_sb[m][:, cols], in0=accs[(m, n)][:], in1=bias_bf[:, cols], op=ALU.add)
+
+        def finish(m, n, eng):
+            cols = slice(n * NH, (n + 1) * NH)
+            if eng == "s":
+                nc.scalar.activation(out=o_sb[m][:, cols], in_=o_sb[m][:, cols], func=ACT.Relu)
             else:
                 nc.gpsimd.tensor_scalar(
-                    out=o_sb[m][:], in0=o_sb[m][:], scalar1=float("inf"), scalar2=0.0, op0=ALU.min, op1=ALU.max
+                    out=o_sb[m][:, cols], in0=o_sb[m][:, cols], scalar1=float("inf"), scalar2=0.0, op0=ALU.min, op1=ALU.max
                 )
-            nc.sync.dma_start(out=out_v[:, m, :], in_=o_sb[m][:])
+            nc.sync.dma_start(out=out_v[:, m, cols], in_=o_sb[m][:, cols])
 
+        A = range(0, 4)
+        B = range(4, 8)
         ln_stats(0)
-        w_prep(0, 0)
+        w_regroup(0, 0, "g")
+        w_regroup(1, 0, "g")
+        ln_rstd(0)
+        ln_norm(0, "s")
         ln_stats(1)
-        ln_apply(0)
-        w_prep(1, 0)
-        w_prep(0, 1)
-        ln_apply(1)
-        w_prep(1, 1)
-        for g in range(2):
-            for n in range(2):
-                for mi in range(4):
-                    mm(4 * g + mi, n)
-            for mi in range(4):
-                finish(4 * g + mi)
+        ln_rstd(1)
+        x_words()
+        w_quant(0, 0)
+        w_quant(1, 0)
+        ln_gain(0)
+        z_quant(0)
+        for m in A:
+            mm(m, 0)
+        w_regroup(0, 1, "s")
+        w_quant(0, 1)
+        ln_norm(1, "g")
+        w_regroup(1, 1, "s")
+        add_bias(0, 0)
+        add_bias(1, 0)
+        add_bias(2, 0)
+        w_quant(1, 1)
+        add_bias(3, 0)
+        for m in A:
+            mm(m, 1)
+        for m in A:
+            finish(m, 0, "g")
+        ln_gain(1)
+        for m in A:
+            add_bias(m, 1)
+        z_quant(1)
+        for m in A:
+            finish(m, 1, "s")
+        for n in range(2):
+            for m in B:
+                mm(m, n)
+            for m in B:
+                add_bias(m, n)
+                finish(m, n, "s" if m % 2 == 0 else "g")

@@ -41,8 +41,8 @@ def tile_edgeupdaterwrapper_v01_pa_kernel(tc, p, x_down, ln_edge_g, ln_edge_b, W
 
     with ExitStack() as ctx:
         const = ctx.enter_context(tc.tile_pool(name="const", bufs=1))
-        ps_tp = ctx.enter_context(tc.psum_pool(name="ps_tp", bufs=1))
-        ps_acc = ctx.enter_context(tc.psum_pool(name="ps_acc", bufs=4))
+        ps_a = ctx.enter_context(tc.psum_pool(name="ps_a", bufs=4))
+        ps_b = ctx.enter_context(tc.psum_pool(name="ps_b", bufs=4))
         ctx.enter_context(tc.manual_schedule())
 
         p_sb = const.tile([P, MT, ED], BF16, name="p_sb")
@@ -118,10 +118,10 @@ def tile_edgeupdaterwrapper_v01_pa_kernel(tc, p, x_down, ln_edge_g, ln_edge_b, W
             in_=ident_b[:, 0:NODES].rearrange("p (a m) -> p m a", a=4).unsqueeze(1).to_broadcast([P, 4, MT, 4]),
         )
 
-        su_ps = ps_acc.tile([P, P], BF16, name="su_ps", tag="acc")
+        su_ps = ps_b.tile([P, P], BF16, name="su_ps", tag="b")
         nc.tensor.transpose(su_ps[:], su[:], ident_b[:])
         nc.scalar.copy(out=gb[:], in_=su_ps[:, 0:8])
-        xp = ps_acc.tile([P, 4, P], F32, name="xp", tag="acc")
+        xp = ps_b.tile([P, 4, P], F32, name="xp", tag="b")
         for t in range(4):
             nc.tensor.matmul(xp[:, t, :], lhsT=xx[:, HD + t : 3 * HD : 4], rhs=sel_i[:], start=True, stop=False)
             nc.tensor.matmul(xp[:, t, :], lhsT=xx[:, t : 2 * HD : 4], rhs=sel_j[:], start=False, stop=True)
@@ -156,9 +156,12 @@ def tile_edgeupdaterwrapper_v01_pa_kernel(tc, p, x_down, ln_edge_g, ln_edge_b, W
                 nc.vector.bn_stats(out=stats[:, m, :], in_=p_sb[:, m, :])
                 nc.vector.bn_aggr(out=mv[:, m, :], in_=stats[:, m, :])
 
-        def ln_rstd(g):
+        def ln_std(g):
             ms = slice(4 * g, 4 * g + 4)
             nc.scalar.activation(out=std[:, ms], in_=mv[:, ms, 1], func=ACT.Sqrt, bias=eps_t[:, 0:1])
+
+        def ln_rstd(g):
+            ms = slice(4 * g, 4 * g + 4)
             nc.vector.reciprocal(out=rstd[:, ms], in_=std[:, ms])
             nc.vector.scalar_tensor_tensor(
                 out=nmr[:, ms], in0=mv[:, ms, 0], scalar=-1.0, in1=rstd[:, ms], op0=ALU.mult, op1=ALU.mult
@@ -166,22 +169,31 @@ def tile_edgeupdaterwrapper_v01_pa_kernel(tc, p, x_down, ln_edge_g, ln_edge_b, W
 
         tps = {}
 
-        def ln_norm(g, eng):
+        def tp_banks(g):
             for t in range(4):
-                tps[(g, t)] = ps_tp.tile([P, 4, P], F32, name="tp%d" % t)
-            for mi in range(4):
-                m = 4 * g + mi
-                if eng == "s":
-                    nc.scalar.activation(
-                        out=xn[m][:], in_=p_sb[:, m, :], func=ACT.Identity, scale=rstd[:, m : m + 1], bias=nmr[:, m : m + 1]
-                    )
+                if g == 0:
+                    tps[(g, t)] = ps_a.tile([P, 4, P], F32, name="tpa", tag="a")
                 else:
-                    nc.gpsimd.tensor_scalar(
-                        out=xn[m][:], in0=p_sb[:, m, :], scalar1=rstd[:, m : m + 1], scalar2=nmr[:, m : m + 1],
-                        op0=ALU.mult, op1=ALU.add,
-                    )
-                for t in range(4):
-                    nc.tensor.transpose(tps[(g, t)][:, mi, :], xn[m][:, t * P : (t + 1) * P], ident_f[:])
+                    tps[(g, t)] = ps_b.tile([P, 4, P], F32, name="tpb", tag="b")
+
+        def ln_norm(m, eng):
+            g = m // 4
+            if eng == "s":
+                nc.scalar.activation(
+                    out=xn[m][:], in_=p_sb[:, m, :], func=ACT.Identity, scale=rstd[:, m : m + 1], bias=nmr[:, m : m + 1]
+                )
+            elif eng == "v":
+                nc.vector.tensor_scalar(
+                    out=xn[m][:], in0=p_sb[:, m, :], scalar1=rstd[:, m : m + 1], scalar2=nmr[:, m : m + 1],
+                    op0=ALU.mult, op1=ALU.add,
+                )
+            else:
+                nc.gpsimd.tensor_scalar(
+                    out=xn[m][:], in0=p_sb[:, m, :], scalar1=rstd[:, m : m + 1], scalar2=nmr[:, m : m + 1],
+                    op0=ALU.mult, op1=ALU.add,
+                )
+            for t in range(4):
+                nc.tensor.transpose(tps[(g, t)][:, m % 4, :], xn[m][:, t * P : (t + 1) * P], ident_f[:])
 
         def ln_gain(g):
             for t in range(4):
@@ -190,8 +202,10 @@ def tile_edgeupdaterwrapper_v01_pa_kernel(tc, p, x_down, ln_edge_g, ln_edge_b, W
                     scale=gb[:, t : t + 1], bias=gb[:, 4 + t : 5 + t],
                 )
 
+        def z_regroup(g, eng):
+            regroup(nc, eng, zg[g][:], zp[g][:])
+
         def z_quant(g):
-            regroup(nc, "v", zg[g][:], zp[g][:])
             cols = slice(g * NH, (g + 1) * NH)
             nc.vector.quantize_mx(
                 out=zc[:, cols].bitcast(FP8X4), scales=zs[:, cols], in_=zg[g][:].rearrange("p w t -> p (w t)")
@@ -211,7 +225,7 @@ def tile_edgeupdaterwrapper_v01_pa_kernel(tc, p, x_down, ln_edge_g, ln_edge_b, W
         def mm(m, n):
             rows = slice(m * P, (m + 1) * P)
             cols = slice(n * NH, (n + 1) * NH)
-            acc = ps_acc.tile([P, NH], F32, name="acc", tag="acc")
+            acc = ps_a.tile([P, NH], F32, name="acc", tag="a")
             accs[(m, n)] = acc
             nc.tensor.matmul_mx(
                 out=acc[:], lhsT=c0[:, rows].bitcast(FP8X4), lhsT_scale=s0[:, rows],
@@ -230,6 +244,8 @@ def tile_edgeupdaterwrapper_v01_pa_kernel(tc, p, x_down, ln_edge_g, ln_edge_b, W
             cols = slice(n * NH, (n + 1) * NH)
             if eng == "s":
                 nc.scalar.activation(out=o_sb[m][:, cols], in_=o_sb[m][:, cols], func=ACT.Relu)
+            elif eng == "v":
+                nc.vector.tensor_scalar_max(out=o_sb[m][:, cols], in0=o_sb[m][:, cols], scalar1=0.0)
             else:
                 nc.gpsimd.tensor_scalar(
                     out=o_sb[m][:, cols], in0=o_sb[m][:, cols], scalar1=float("inf"), scalar2=0.0, op0=ALU.min, op1=ALU.max
@@ -238,37 +254,45 @@ def tile_edgeupdaterwrapper_v01_pa_kernel(tc, p, x_down, ln_edge_g, ln_edge_b, W
 
         A = range(0, 4)
         B = range(4, 8)
+        tp_banks(0)
+        tp_banks(1)
         ln_stats(0)
-        w_regroup(0, 0, "g")
-        w_regroup(1, 0, "g")
+        w_regroup(0, 0, "s")
+        ln_std(0)
+        w_regroup(1, 0, "v")
         ln_rstd(0)
-        ln_norm(0, "s")
+        for m in A:
+            ln_norm(m, "s")
         ln_stats(1)
-        ln_rstd(1)
         x_words()
+        ln_std(1)
+        ln_rstd(1)
         w_quant(0, 0)
         w_quant(1, 0)
+        w_regroup(0, 1, "v")
         ln_gain(0)
+        for m in B:
+            ln_norm(m, "s")
+        z_regroup(0, "v")
         z_quant(0)
         for m in A:
             mm(m, 0)
-        w_regroup(0, 1, "s")
+        w_regroup(1, 1, "v")
         w_quant(0, 1)
-        ln_norm(1, "g")
-        w_regroup(1, 1, "s")
-        add_bias(0, 0)
-        add_bias(1, 0)
-        add_bias(2, 0)
         w_quant(1, 1)
-        add_bias(3, 0)
+        ln_gain(1)
+        z_regroup(1, "s")
+        for m in A:
+            add_bias(m, 0)
         for m in A:
             mm(m, 1)
         for m in A:
-            finish(m, 0, "g")
-        ln_gain(1)
-        for m in A:
-            add_bias(m, 1)
+            finish(m, 0, "s")
+        add_bias(0, 1)
+        add_bias(1, 1)
         z_quant(1)
+        add_bias(2, 1)
+        add_bias(3, 1)
         for m in A:
             finish(m, 1, "s")
         for n in range(2):
@@ -276,4 +300,4 @@ def tile_edgeupdaterwrapper_v01_pa_kernel(tc, p, x_down, ln_edge_g, ln_edge_b, W
                 mm(m, n)
             for m in B:
                 add_bias(m, n)
-                finish(m, n, "s" if m % 2 == 0 else "g")
+                finish(m, n, "s")

@@ -23,7 +23,7 @@ EPS = 1e-5
 FLOPS = 2 * 1024 * 1024 * 1024
 
 
-def regroup(nc, eng, dst, src):
+def regroup(nc, eng, dst, src, one=1.0):
     dv = dst.rearrange("p (c i) t -> p c t i", i=4)
     sv = src.rearrange("p t (c i) -> p c t i", i=4)
     if eng == "v":
@@ -31,7 +31,7 @@ def regroup(nc, eng, dst, src):
     elif eng == "s":
         nc.scalar.copy(out=dv, in_=sv)
     else:
-        nc.gpsimd.tensor_scalar(out=dv, in0=sv, scalar1=1.0, scalar2=0.0, op0=ALU.mult, op1=ALU.add)
+        nc.gpsimd.tensor_scalar(out=dv, in0=sv, scalar1=one, scalar2=0.0, op0=ALU.mult, op1=ALU.add)
 
 
 def tile_edgeupdaterwrapper_v01_pa_kernel(tc, p, x_down, ln_edge_g, ln_edge_b, W1, b1, out):
@@ -52,6 +52,7 @@ def tile_edgeupdaterwrapper_v01_pa_kernel(tc, p, x_down, ln_edge_g, ln_edge_b, W
             for n in range(2):
                 wraw[(c, n)] = const.tile([P, 4, NH], BF16, name="wraw%d%d" % (c, n))
                 wg[(c, n)] = const.tile([P, NH, 4], BF16, name="wg%d%d" % (c, n), align_bytes=64)
+        token = const.tile([P, 1], F32, name="token")
         eps_t = const.tile([P, 1], F32, name="eps_t")
         junk = const.tile([P, 1], F32, name="junk")
         xx = const.tile([P, 3 * HD], BF16, name="xx")
@@ -69,7 +70,6 @@ def tile_edgeupdaterwrapper_v01_pa_kernel(tc, p, x_down, ln_edge_g, ln_edge_b, W
         s0 = const.tile([P, MT * P], U8, name="s0", align_bytes=64)
         stats = const.tile([P, MT, 6], F32, name="stats")
         mv = const.tile([P, MT, 2], F32, name="mv")
-        std = const.tile([P, MT], F32, name="std")
         rstd = const.tile([P, MT], F32, name="rstd")
         nmr = const.tile([P, MT], F32, name="nmr")
         zc = const.tile([P, MT * P], U32, name="zc", align_bytes=64)
@@ -86,7 +86,7 @@ def tile_edgeupdaterwrapper_v01_pa_kernel(tc, p, x_down, ln_edge_g, ln_edge_b, W
         nc.vector.memset(eps_t[:], EPS)
         nc.vector.memset(xs[:].bitcast(I32), 0)
         make_identity(nc, ident_f[:])
-        nc.scalar.activation(out=junk[:], in_=eps_t[:], func=ACT.Sqrt)
+        nc.scalar.activation(out=junk[:], in_=eps_t[:], func=ACT.Abs_reciprocal_sqrt)
 
         def load_w(c, n):
             cols = slice(n * NH, (n + 1) * NH)
@@ -96,16 +96,21 @@ def tile_edgeupdaterwrapper_v01_pa_kernel(tc, p, x_down, ln_edge_g, ln_edge_b, W
                 src = W1[512:1024, cols].rearrange("(t q) w -> q t w", q=P)
             nc.sync.dma_start(out=wraw[(c, n)][:], in_=src)
 
-        nc.sync.dma_start(out=p_sb[:, 0:2, :], in_=p_v[:, 0:2, :])
+        def load_p(a, b):
+            nc.sync.dma_start(out=p_sb[:, a:b, :], in_=p_v[:, a:b, :])
+
+        load_p(0, 1)
+        load_p(1, 2)
+        load_w(0, 0)
+        load_p(2, 3)
+        load_p(3, 5)
         nc.sync.dma_start(out=xx[0:NODES, HD : 2 * HD], in_=x_down.rearrange("b n k -> (b n) k"))
         nc.sync.dma_start(out=su[0:4, :], in_=ln_edge_g.rearrange("(t q) -> t q", q=P))
         nc.sync.dma_start(out=su[4:8, :], in_=ln_edge_b.rearrange("(t q) -> t q", q=P))
-        load_w(0, 0)
-        nc.sync.dma_start(out=p_sb[:, 2:4, :], in_=p_v[:, 2:4, :])
         load_w(1, 0)
-        nc.sync.dma_start(out=p_sb[:, 4:8, :], in_=p_v[:, 4:8, :])
-        load_w(0, 1)
+        load_p(5, 8)
         load_w(1, 1)
+        load_w(0, 1)
         nc.sync.dma_start(out=bias_bf[:], in_=b1.partition_broadcast(P))
 
         nc.vector.tensor_copy(out=ident_b[:], in_=ident_f[:])
@@ -120,12 +125,14 @@ def tile_edgeupdaterwrapper_v01_pa_kernel(tc, p, x_down, ln_edge_g, ln_edge_b, W
 
         su_ps = ps_b.tile([P, P], BF16, name="su_ps", tag="b")
         nc.tensor.transpose(su_ps[:], su[:], ident_b[:])
-        nc.scalar.copy(out=gb[:], in_=su_ps[:, 0:8])
         xp = ps_b.tile([P, 4, P], F32, name="xp", tag="b")
         for t in range(4):
             nc.tensor.matmul(xp[:, t, :], lhsT=xx[:, HD + t : 3 * HD : 4], rhs=sel_i[:], start=True, stop=False)
             nc.tensor.matmul(xp[:, t, :], lhsT=xx[:, t : 2 * HD : 4], rhs=sel_j[:], start=False, stop=True)
-        nc.scalar.copy(out=xg[:], in_=xp[:].rearrange("p t c -> p c t"))
+
+        def x_copy():
+            nc.scalar.copy(out=gb[:], in_=su_ps[:, 0:8])
+            nc.scalar.copy(out=xg[:], in_=xp[:].rearrange("p t c -> p c t"))
 
         def x_words():
             nc.vector.quantize_mx(out=xc[:].bitcast(FP8X4), scales=xs[:], in_=xg[:].rearrange("p c t -> p (c t)"))
@@ -134,7 +141,7 @@ def tile_edgeupdaterwrapper_v01_pa_kernel(tc, p, x_down, ln_edge_g, ln_edge_b, W
             c0_i = c0[:].bitcast(I32)
             s0_i = s0[:].bitcast(I32)
             H = 64
-            nc.vector.tensor_copy(
+            nc.sync.dma_start(
                 out=c0_i[0:H, :].rearrange("p (m c) -> p m c", m=MT),
                 in_=xc_i[0:H, :].unsqueeze(1).to_broadcast([H, MT, P]),
             )
@@ -142,7 +149,7 @@ def tile_edgeupdaterwrapper_v01_pa_kernel(tc, p, x_down, ln_edge_g, ln_edge_b, W
                 out=c0_i[H:P, :].rearrange("p (m r a) -> p m r a", m=MT, a=4),
                 in_=xc_i[H:P, 0:32].rearrange("p (m a) -> p m a", a=4).unsqueeze(2).to_broadcast([H, MT, 32, 4]),
             )
-            nc.vector.tensor_copy(
+            nc.sync.dma_start(
                 out=s0_i[0:H, :].rearrange("p (m c) -> p m c", m=MT),
                 in_=xs_i[0:H, :].unsqueeze(1).to_broadcast([H, MT, 32]),
             )
@@ -151,18 +158,20 @@ def tile_edgeupdaterwrapper_v01_pa_kernel(tc, p, x_down, ln_edge_g, ln_edge_b, W
                 in_=xs_i[H:P, 0:MT].unsqueeze(2).to_broadcast([H, MT, 32]),
             )
 
+        def stat1(m):
+            nc.vector.bn_stats(out=stats[:, m, :], in_=p_sb[:, m, :])
+            nc.vector.bn_aggr(out=mv[:, m, :], in_=stats[:, m, :])
+
         def ln_stats(g):
             for m in range(4 * g, 4 * g + 4):
-                nc.vector.bn_stats(out=stats[:, m, :], in_=p_sb[:, m, :])
-                nc.vector.bn_aggr(out=mv[:, m, :], in_=stats[:, m, :])
-
-        def ln_std(g):
-            ms = slice(4 * g, 4 * g + 4)
-            nc.scalar.activation(out=std[:, ms], in_=mv[:, ms, 1], func=ACT.Sqrt, bias=eps_t[:, 0:1])
+                stat1(m)
 
         def ln_rstd(g):
             ms = slice(4 * g, 4 * g + 4)
-            nc.vector.reciprocal(out=rstd[:, ms], in_=std[:, ms])
+            nc.scalar.activation(out=rstd[:, ms], in_=mv[:, ms, 1], func=ACT.Abs_reciprocal_sqrt, bias=eps_t[:, 0:1])
+
+        def ln_shift(g):
+            ms = slice(4 * g, 4 * g + 4)
             nc.vector.scalar_tensor_tensor(
                 out=nmr[:, ms], in0=mv[:, ms, 0], scalar=-1.0, in1=rstd[:, ms], op0=ALU.mult, op1=ALU.mult
             )
@@ -184,8 +193,8 @@ def tile_edgeupdaterwrapper_v01_pa_kernel(tc, p, x_down, ln_edge_g, ln_edge_b, W
                 )
             elif eng == "v":
                 nc.vector.tensor_scalar(
-                    out=xn[m][:], in0=p_sb[:, m, :], scalar1=rstd[:, m : m + 1], scalar2=nmr[:, m : m + 1],
-                    op0=ALU.mult, op1=ALU.add,
+                    out=xn[m][:], in0=p_sb[:, m, :], scalar1=mv[:, m, 0:1], scalar2=rstd[:, m : m + 1],
+                    op0=ALU.subtract, op1=ALU.mult,
                 )
             else:
                 nc.gpsimd.tensor_scalar(
@@ -211,8 +220,8 @@ def tile_edgeupdaterwrapper_v01_pa_kernel(tc, p, x_down, ln_edge_g, ln_edge_b, W
                 out=zc[:, cols].bitcast(FP8X4), scales=zs[:, cols], in_=zg[g][:].rearrange("p w t -> p (w t)")
             )
 
-        def w_regroup(c, n, eng):
-            regroup(nc, eng, wg[(c, n)][:], wraw[(c, n)][:])
+        def w_regroup(c, n, eng, one=1.0):
+            regroup(nc, eng, wg[(c, n)][:], wraw[(c, n)][:], one)
 
         def w_quant(c, n):
             cols = slice(n * NH, (n + 1) * NH)
@@ -220,13 +229,22 @@ def tile_edgeupdaterwrapper_v01_pa_kernel(tc, p, x_down, ln_edge_g, ln_edge_b, W
                 out=wc[c][:, cols].bitcast(FP8X4), scales=ws[c][:, cols], in_=wg[(c, n)][:].rearrange("p w t -> p (w t)")
             )
 
+        def warm(k, dst):
+            for rep in range(k):
+                nc.tensor.matmul(dst, lhsT=ident_f[:], rhs=ident_f[:], start=True, stop=True)
+
         accs = {}
+
+        def acc_bank(m, n):
+            if m < 4:
+                accs[(m, n)] = ps_a.tile([P, NH], F32, name="acc", tag="a")
+            else:
+                accs[(m, n)] = ps_b.tile([P, NH], F32, name="acc", tag="b")
 
         def mm(m, n):
             rows = slice(m * P, (m + 1) * P)
             cols = slice(n * NH, (n + 1) * NH)
-            acc = ps_a.tile([P, NH], F32, name="acc", tag="a")
-            accs[(m, n)] = acc
+            acc = accs[(m, n)]
             nc.tensor.matmul_mx(
                 out=acc[:], lhsT=c0[:, rows].bitcast(FP8X4), lhsT_scale=s0[:, rows],
                 rhs=wc[0][:, cols].bitcast(FP8X4), rhs_scale=ws[0][:, cols], start=True, stop=False,
@@ -254,50 +272,57 @@ def tile_edgeupdaterwrapper_v01_pa_kernel(tc, p, x_down, ln_edge_g, ln_edge_b, W
 
         A = range(0, 4)
         B = range(4, 8)
-        tp_banks(0)
-        tp_banks(1)
+        w_regroup(0, 0, "g")
         ln_stats(0)
-        w_regroup(0, 0, "s")
-        ln_std(0)
-        w_regroup(1, 0, "v")
         ln_rstd(0)
+        w_regroup(1, 0, "s")
+        stat1(4)
+        tp_banks(0)
         for m in A:
-            ln_norm(m, "s")
-        ln_stats(1)
-        x_words()
-        ln_std(1)
+            ln_norm(m, "v")
+        nc.vector.memset(token[:], 1.0)
+        w_regroup(1, 1, "g", token[:, 0:1])
+        x_copy()
+        stat1(5)
+        stat1(6)
+        stat1(7)
+        ln_gain(0)
         ln_rstd(1)
         w_quant(0, 0)
         w_quant(1, 0)
-        w_regroup(0, 1, "v")
-        ln_gain(0)
+        ln_shift(1)
+        x_words()
+        tp_banks(1)
         for m in B:
             ln_norm(m, "s")
         z_regroup(0, "v")
         z_quant(0)
         for m in A:
+            acc_bank(m, 0)
+        for m in A:
             mm(m, 0)
-        w_regroup(1, 1, "v")
+        ln_gain(1)
+        w_regroup(0, 1, "v")
         w_quant(0, 1)
         w_quant(1, 1)
-        ln_gain(1)
-        z_regroup(1, "s")
+        z_regroup(1, "g")
         for m in A:
             add_bias(m, 0)
-        for m in A:
-            mm(m, 1)
-        for m in A:
             finish(m, 0, "s")
+        for m in A:
+            acc_bank(m, 1)
+            mm(m, 1)
         add_bias(0, 1)
         add_bias(1, 1)
         z_quant(1)
         add_bias(2, 1)
         add_bias(3, 1)
         for m in A:
-            finish(m, 1, "s")
+            finish(m, 1, "gs"[m % 2])
         for n in range(2):
             for m in B:
+                acc_bank(m, n)
                 mm(m, n)
             for m in B:
                 add_bias(m, n)
-                finish(m, n, "s")
+                finish(m, n, "gs"[m % 2])

@@ -23,9 +23,9 @@ EPS = 1e-5
 FLOPS = 2 * 1024 * 1024 * 1024
 
 
-def regroup(nc, eng, dst, src, one=1.0):
-    dv = dst.rearrange("p (c i) t -> p c t i", i=4)
-    sv = src.rearrange("p t (c i) -> p c t i", i=4)
+def regroup(nc, eng, dst, src, one=1.0, cols=slice(0, NH)):
+    dv = dst[:, cols, :].rearrange("p (c i) t -> p c t i", i=4)
+    sv = src[:, :, cols].rearrange("p t (c i) -> p c t i", i=4)
     if eng == "v":
         nc.vector.tensor_copy(out=dv, in_=sv)
     elif eng == "s":
@@ -70,6 +70,7 @@ def tile_edgeupdaterwrapper_v01_pa_kernel(tc, p, x_down, ln_edge_g, ln_edge_b, W
         s0 = const.tile([P, MT * P], U8, name="s0", align_bytes=64)
         stats = const.tile([P, MT, 6], F32, name="stats")
         mv = const.tile([P, MT, 2], F32, name="mv")
+        ssq = const.tile([P, MT], F32, name="ssq")
         rstd = const.tile([P, MT], F32, name="rstd")
         nmr = const.tile([P, MT], F32, name="nmr")
         zc = const.tile([P, MT * P], U32, name="zc", align_bytes=64)
@@ -101,14 +102,15 @@ def tile_edgeupdaterwrapper_v01_pa_kernel(tc, p, x_down, ln_edge_g, ln_edge_b, W
 
         load_p(0, 1)
         load_p(1, 2)
-        load_w(0, 0)
-        load_p(2, 3)
-        load_p(3, 5)
         nc.sync.dma_start(out=xx[0:NODES, HD : 2 * HD], in_=x_down.rearrange("b n k -> (b n) k"))
+        load_p(2, 3)
+        load_w(0, 0)
+        load_p(3, 4)
+        load_p(4, 6)
         nc.sync.dma_start(out=su[0:4, :], in_=ln_edge_g.rearrange("(t q) -> t q", q=P))
         nc.sync.dma_start(out=su[4:8, :], in_=ln_edge_b.rearrange("(t q) -> t q", q=P))
         load_w(1, 0)
-        load_p(5, 8)
+        load_p(6, 8)
         load_w(1, 1)
         load_w(0, 1)
         nc.sync.dma_start(out=bias_bf[:], in_=b1.partition_broadcast(P))
@@ -119,19 +121,21 @@ def tile_edgeupdaterwrapper_v01_pa_kernel(tc, p, x_down, ln_edge_g, ln_edge_b, W
             in_=ident_b[:, 0:NODES].unsqueeze(2).to_broadcast([P, NODES, 4]),
         )
         nc.vector.tensor_copy(
-            out=sel_j[:].rearrange("p (r m a) -> p r m a", r=4, a=4),
-            in_=ident_b[:, 0:NODES].rearrange("p (a m) -> p m a", a=4).unsqueeze(1).to_broadcast([P, 4, MT, 4]),
+            out=sel_j[:].rearrange("p (m r a) -> p m r a", r=4, a=4),
+            in_=ident_b[:, 0:NODES].rearrange("p (a m) -> p m a", a=4).unsqueeze(2).to_broadcast([P, MT, 4, 4]),
         )
 
-        su_ps = ps_b.tile([P, P], BF16, name="su_ps", tag="b")
-        nc.tensor.transpose(su_ps[:], su[:], ident_b[:])
         xp = ps_b.tile([P, 4, P], F32, name="xp", tag="b")
         for t in range(4):
             nc.tensor.matmul(xp[:, t, :], lhsT=xx[:, HD + t : 3 * HD : 4], rhs=sel_i[:], start=True, stop=False)
             nc.tensor.matmul(xp[:, t, :], lhsT=xx[:, t : 2 * HD : 4], rhs=sel_j[:], start=False, stop=True)
+        su_ps = ps_b.tile([P, P], BF16, name="su_ps", tag="b")
+        nc.tensor.transpose(su_ps[:], su[:], ident_b[:])
+
+        def g_copy():
+            nc.scalar.copy(out=gb[:], in_=su_ps[:, 0:8])
 
         def x_copy():
-            nc.scalar.copy(out=gb[:], in_=su_ps[:, 0:8])
             nc.scalar.copy(out=xg[:], in_=xp[:].rearrange("p t c -> p c t"))
 
         def x_words():
@@ -145,22 +149,38 @@ def tile_edgeupdaterwrapper_v01_pa_kernel(tc, p, x_down, ln_edge_g, ln_edge_b, W
                 out=c0_i[0:H, :].rearrange("p (m c) -> p m c", m=MT),
                 in_=xc_i[0:H, :].unsqueeze(1).to_broadcast([H, MT, P]),
             )
-            nc.vector.tensor_copy(
-                out=c0_i[H:P, :].rearrange("p (m r a) -> p m r a", m=MT, a=4),
-                in_=xc_i[H:P, 0:32].rearrange("p (m a) -> p m a", a=4).unsqueeze(2).to_broadcast([H, MT, 32, 4]),
-            )
             nc.sync.dma_start(
                 out=s0_i[0:H, :].rearrange("p (m c) -> p m c", m=MT),
                 in_=xs_i[0:H, :].unsqueeze(1).to_broadcast([H, MT, 32]),
             )
+            for m in range(MT):
+                nc.sync.dma_start(
+                    out=c0_i[H:P, m * P : (m + 1) * P].rearrange("p (r c) -> p r c", r=8),
+                    in_=xc_i[H:P, m * 16 : (m + 1) * 16].unsqueeze(1).to_broadcast([H, 8, 16]),
+                )
             nc.vector.tensor_copy(
-                out=s0_i[H:P, :].rearrange("p (m r) -> p m r", m=MT),
-                in_=xs_i[H:P, 0:MT].unsqueeze(2).to_broadcast([H, MT, 32]),
+                out=s0_i[H:P, :].rearrange("p (m r a) -> p m r a", m=MT, a=4),
+                in_=xs_i[H:P, :].rearrange("p (m a) -> p m a", m=MT).unsqueeze(2).to_broadcast([H, MT, 8, 4]),
             )
 
         def stat1(m):
             nc.vector.bn_stats(out=stats[:, m, :], in_=p_sb[:, m, :])
             nc.vector.bn_aggr(out=mv[:, m, :], in_=stats[:, m, :])
+
+        def stat_s(m):
+            nc.scalar.activation(
+                out=xn[m][:], in_=p_sb[:, m, :], func=ACT.Identity, scale=1.0 / ED, accum_out=mv[:, m, 0:1]
+            )
+            nc.scalar.activation(
+                out=xn[m][:], in_=p_sb[:, m, :], func=ACT.Square, scale=-1.0, bias=mv[:, m, 0:1], accum_out=ssq[:, m : m + 1]
+            )
+            nc.scalar.activation(out=mv[:, m, 1:2], in_=ssq[:, m : m + 1], func=ACT.Identity, scale=1.0 / ED)
+
+        def shift1(m):
+            nc.vector.tensor_scalar(
+                out=nmr[:, m : m + 1], in0=mv[:, m, 0:1], scalar1=rstd[:, m : m + 1], scalar2=-1.0,
+                op0=ALU.mult, op1=ALU.mult,
+            )
 
         def ln_stats(g):
             for m in range(4 * g, 4 * g + 4):
@@ -201,18 +221,26 @@ def tile_edgeupdaterwrapper_v01_pa_kernel(tc, p, x_down, ln_edge_g, ln_edge_b, W
                     out=xn[m][:], in0=p_sb[:, m, :], scalar1=rstd[:, m : m + 1], scalar2=nmr[:, m : m + 1],
                     op0=ALU.mult, op1=ALU.add,
                 )
-            for t in range(4):
-                nc.tensor.transpose(tps[(g, t)][:, m % 4, :], xn[m][:, t * P : (t + 1) * P], ident_f[:])
 
-        def ln_gain(g):
+        def ln_turn(m):
             for t in range(4):
+                nc.tensor.transpose(tps[(m // 4, t)][:, m % 4, :], xn[m][:, t * P : (t + 1) * P], ident_f[:])
+
+        def gain_v(g, t):
+            nc.vector.tensor_scalar(
+                out=zp[g][:, t, :], in0=tps[(g, t)][:].rearrange("p m c -> p (m c)"),
+                scalar1=gb[:, t : t + 1], scalar2=gb[:, 4 + t : 5 + t], op0=ALU.mult, op1=ALU.add,
+            )
+
+        def ln_gain(g, ts=range(4)):
+            for t in ts:
                 nc.scalar.activation(
                     out=zp[g][:, t, :], in_=tps[(g, t)][:].rearrange("p m c -> p (m c)"), func=ACT.Identity,
                     scale=gb[:, t : t + 1], bias=gb[:, 4 + t : 5 + t],
                 )
 
-        def z_regroup(g, eng):
-            regroup(nc, eng, zg[g][:], zp[g][:])
+        def z_regroup(g, eng, cols=slice(0, NH)):
+            regroup(nc, eng, zg[g][:], zp[g][:], 1.0, cols)
 
         def z_quant(g):
             cols = slice(g * NH, (g + 1) * NH)
@@ -220,8 +248,8 @@ def tile_edgeupdaterwrapper_v01_pa_kernel(tc, p, x_down, ln_edge_g, ln_edge_b, W
                 out=zc[:, cols].bitcast(FP8X4), scales=zs[:, cols], in_=zg[g][:].rearrange("p w t -> p (w t)")
             )
 
-        def w_regroup(c, n, eng, one=1.0):
-            regroup(nc, eng, wg[(c, n)][:], wraw[(c, n)][:], one)
+        def w_regroup(c, n, eng, one=1.0, cols=slice(0, NH)):
+            regroup(nc, eng, wg[(c, n)][:], wraw[(c, n)][:], one, cols)
 
         def w_quant(c, n):
             cols = slice(n * NH, (n + 1) * NH)
@@ -236,7 +264,7 @@ def tile_edgeupdaterwrapper_v01_pa_kernel(tc, p, x_down, ln_edge_g, ln_edge_b, W
         accs = {}
 
         def acc_bank(m, n):
-            if m < 4:
+            if m < 4 or n == 1:
                 accs[(m, n)] = ps_a.tile([P, NH], F32, name="acc", tag="a")
             else:
                 accs[(m, n)] = ps_b.tile([P, NH], F32, name="acc", tag="b")
@@ -258,6 +286,11 @@ def tile_edgeupdaterwrapper_v01_pa_kernel(tc, p, x_down, ln_edge_g, ln_edge_b, W
             cols = slice(n * NH, (n + 1) * NH)
             nc.vector.tensor_tensor(out=o_sb[m][:, cols], in0=accs[(m, n)][:], in1=bias_bf[:, cols], op=ALU.add)
 
+        def add_bias_g(m, n):
+            cols = slice(n * NH, (n + 1) * NH)
+            nc.scalar.copy(out=o_sb[m][:, cols], in_=accs[(m, n)][:])
+            nc.gpsimd.tensor_tensor(out=o_sb[m][:, cols], in0=o_sb[m][:, cols], in1=bias_bf[:, cols], op=ALU.add)
+
         def finish(m, n, eng):
             cols = slice(n * NH, (n + 1) * NH)
             if eng == "s":
@@ -272,52 +305,60 @@ def tile_edgeupdaterwrapper_v01_pa_kernel(tc, p, x_down, ln_edge_g, ln_edge_b, W
 
         A = range(0, 4)
         B = range(4, 8)
+        lo, hi = slice(0, NH // 2), slice(NH // 2, NH)
         w_regroup(0, 0, "g")
-        ln_stats(0)
+        stat1(0)
+        stat_s(1)
+        x_copy()
+        stat1(2)
+        stat1(3)
         ln_rstd(0)
         w_regroup(1, 0, "s")
         stat1(4)
+        stat1(5)
         tp_banks(0)
+        warm(3, tps[(0, 3)][:, 3, :])
         for m in A:
             ln_norm(m, "v")
+            ln_turn(m)
         nc.vector.memset(token[:], 1.0)
-        w_regroup(1, 1, "g", token[:, 0:1])
-        x_copy()
-        stat1(5)
+        w_regroup(1, 1, "g", token[:, 0:1], lo)
+        g_copy()
         stat1(6)
         stat1(7)
-        ln_gain(0)
+        ln_gain(0, (0, 1))
         ln_rstd(1)
-        w_quant(0, 0)
-        w_quant(1, 0)
-        ln_shift(1)
+        ln_gain(0, (2, 3))
         x_words()
+        w_quant(0, 0)
+        ln_shift(1)
+        w_quant(1, 0)
         tp_banks(1)
         for m in B:
             ln_norm(m, "s")
+            ln_turn(m)
         z_regroup(0, "v")
         z_quant(0)
+        w_regroup(1, 1, "s", 1.0, hi)
         for m in A:
             acc_bank(m, 0)
         for m in A:
             mm(m, 0)
         ln_gain(1)
         w_regroup(0, 1, "v")
-        w_quant(0, 1)
         w_quant(1, 1)
-        z_regroup(1, "g")
+        w_quant(0, 1)
+        z_regroup(1, "g", lo)
+        z_regroup(1, "s", hi)
         for m in A:
             add_bias(m, 0)
             finish(m, 0, "s")
         for m in A:
             acc_bank(m, 1)
             mm(m, 1)
-        add_bias(0, 1)
-        add_bias(1, 1)
         z_quant(1)
-        add_bias(2, 1)
-        add_bias(3, 1)
         for m in A:
+            add_bias(m, 1)
             finish(m, 1, "gs"[m % 2])
         for n in range(2):
             for m in B:

@@ -158,13 +158,20 @@ def tile_edgeupdaterwrapper_v01_pa_kernel(tc, p, x_down, ln_edge_g, ln_edge_b, W
                     out=c0_i[H:P, m * P : (m + 1) * P].rearrange("p (r c) -> p r c", r=8),
                     in_=xc_i[H:P, m * 16 : (m + 1) * 16].unsqueeze(1).to_broadcast([H, 8, 16]),
                 )
+
+        def x_scales():
+            H = 64
+            xs_i = xs[:].bitcast(I32)
+            s0_i = s0[:].bitcast(I32)
             nc.vector.tensor_copy(
                 out=s0_i[H:P, :].rearrange("p (m r a) -> p m r a", m=MT, a=4),
                 in_=xs_i[H:P, :].rearrange("p (m a) -> p m a", m=MT).unsqueeze(2).to_broadcast([H, MT, 8, 4]),
             )
 
-        def stat1(m):
+        def bs(m):
             nc.vector.bn_stats(out=stats[:, m, :], in_=p_sb[:, m, :])
+
+        def ba(m):
             nc.vector.bn_aggr(out=mv[:, m, :], in_=stats[:, m, :])
 
         def stat_s(m):
@@ -181,10 +188,6 @@ def tile_edgeupdaterwrapper_v01_pa_kernel(tc, p, x_down, ln_edge_g, ln_edge_b, W
                 out=nmr[:, m : m + 1], in0=mv[:, m, 0:1], scalar1=rstd[:, m : m + 1], scalar2=-1.0,
                 op0=ALU.mult, op1=ALU.mult,
             )
-
-        def ln_stats(g):
-            for m in range(4 * g, 4 * g + 4):
-                stat1(m)
 
         def ln_rstd(g):
             ms = slice(4 * g, 4 * g + 4)
@@ -282,17 +285,17 @@ def tile_edgeupdaterwrapper_v01_pa_kernel(tc, p, x_down, ln_edge_g, ln_edge_b, W
                 rhs=wc[1][:, cols].bitcast(FP8X4), rhs_scale=ws[1][:, cols], start=False, stop=True,
             )
 
-        def add_bias(m, n):
-            cols = slice(n * NH, (n + 1) * NH)
-            nc.vector.tensor_tensor(out=o_sb[m][:, cols], in0=accs[(m, n)][:], in1=bias_bf[:, cols], op=ALU.add)
+        def add_bias(m, n, a=0, b=NH):
+            cols = slice(n * NH + a, n * NH + b)
+            nc.vector.tensor_tensor(out=o_sb[m][:, cols], in0=accs[(m, n)][:, a:b], in1=bias_bf[:, cols], op=ALU.add)
 
         def add_bias_g(m, n):
             cols = slice(n * NH, (n + 1) * NH)
             nc.scalar.copy(out=o_sb[m][:, cols], in_=accs[(m, n)][:])
             nc.gpsimd.tensor_tensor(out=o_sb[m][:, cols], in0=o_sb[m][:, cols], in1=bias_bf[:, cols], op=ALU.add)
 
-        def finish(m, n, eng):
-            cols = slice(n * NH, (n + 1) * NH)
+        def finish(m, n, eng, a=0, b=NH):
+            cols = slice(n * NH + a, n * NH + b)
             if eng == "s":
                 nc.scalar.activation(out=o_sb[m][:, cols], in_=o_sb[m][:, cols], func=ACT.Relu)
             elif eng == "v":
@@ -307,15 +310,20 @@ def tile_edgeupdaterwrapper_v01_pa_kernel(tc, p, x_down, ln_edge_g, ln_edge_b, W
         B = range(4, 8)
         lo, hi = slice(0, NH // 2), slice(NH // 2, NH)
         w_regroup(0, 0, "g")
-        stat1(0)
+        bs(0)
         stat_s(1)
         x_copy()
-        stat1(2)
-        stat1(3)
+        bs(2)
+        ba(0)
+        ba(2)
+        bs(3)
+        ba(3)
         ln_rstd(0)
         w_regroup(1, 0, "s")
-        stat1(4)
-        stat1(5)
+        bs(4)
+        bs(5)
+        ba(4)
+        ba(5)
         tp_banks(0)
         warm(3, tps[(0, 3)][:, 3, :])
         for m in A:
@@ -324,20 +332,24 @@ def tile_edgeupdaterwrapper_v01_pa_kernel(tc, p, x_down, ln_edge_g, ln_edge_b, W
         nc.vector.memset(token[:], 1.0)
         w_regroup(1, 1, "g", token[:, 0:1], lo)
         g_copy()
-        stat1(6)
-        stat1(7)
+        bs(6)
+        bs(7)
+        ba(6)
+        ba(7)
         ln_gain(0, (0, 1))
         ln_rstd(1)
-        ln_gain(0, (2, 3))
+        ln_gain(0, (2,))
         x_words()
         w_quant(0, 0)
         ln_shift(1)
-        w_quant(1, 0)
+        x_scales()
+        gain_v(0, 3)
         tp_banks(1)
         for m in B:
             ln_norm(m, "s")
             ln_turn(m)
         z_regroup(0, "v")
+        w_quant(1, 0)
         z_quant(0)
         w_regroup(1, 1, "s", 1.0, hi)
         for m in A:
@@ -365,5 +377,6 @@ def tile_edgeupdaterwrapper_v01_pa_kernel(tc, p, x_down, ln_edge_g, ln_edge_b, W
                 acc_bank(m, n)
                 mm(m, n)
             for m in B:
-                add_bias(m, n)
-                finish(m, n, "gs"[m % 2])
+                for a, b in [(0, NH // 2), (NH // 2, NH)] if (m, n) == (7, 1) else [(0, NH)]:
+                    add_bias(m, n, a, b)
+                    finish(m, n, "gs"[m % 2], a, b)

@@ -319,6 +319,7 @@ def tile_edgeupdaterwrapper_v01_pa_kernel(tc, p, x_down, ln_edge_g, ln_edge_b, W
         bs(3)
         ba(3)
         ln_rstd(0)
+        g_copy()
         w_regroup(1, 0, "s")
         bs(4)
         bs(5)
@@ -331,7 +332,6 @@ def tile_edgeupdaterwrapper_v01_pa_kernel(tc, p, x_down, ln_edge_g, ln_edge_b, W
             ln_turn(m)
         nc.vector.memset(token[:], 1.0)
         w_regroup(1, 1, "g", token[:, 0:1], lo)
-        g_copy()
         bs(6)
         bs(7)
         ba(6)
@@ -364,19 +364,24 @@ def tile_edgeupdaterwrapper_v01_pa_kernel(tc, p, x_down, ln_edge_g, ln_edge_b, W
         z_regroup(1, "s", hi)
         for m in A:
             add_bias(m, 0)
-            finish(m, 0, "s")
+            finish(m, 0, "ssss"[m])
         for m in A:
             acc_bank(m, 1)
             mm(m, 1)
         z_quant(1)
         for m in A:
             add_bias(m, 1)
-            finish(m, 1, "gs"[m % 2])
+            finish(m, 1, "gsgs"[m])
         for n in range(2):
             for m in B:
                 acc_bank(m, n)
                 mm(m, n)
             for m in B:
-                for a, b in [(0, NH // 2), (NH // 2, NH)] if (m, n) == (7, 1) else [(0, NH)]:
-                    add_bias(m, n, a, b)
-                    finish(m, n, "gs"[m % 2], a, b)
+                if (m, n) == (7, 1):
+                    add_bias(m, n, 0, NH // 2)
+                    finish(m, n, "s", 0, NH // 2)
+                    add_bias(m, n, NH // 2, NH)
+                    finish(m, n, "s", NH // 2, NH)
+                else:
+                    add_bias(m, n)
+                    finish(m, n, ("sgss", "gssss")[n][m - 4])

from contextlib import ExitStack

import concourse.mybir as mybir
from concourse.masks import make_identity

F32 = mybir.dt.float32
BF16 = mybir.dt.bfloat16
I32 = mybir.dt.int32
U32 = mybir.dt.uint32
U8 = mybir.dt.uint8
FP8X4 = mybir.dt.float8_e4m3fn_x4
ALU = mybir.AluOpType
ACT = mybir.ActivationFunctionType

P = 128
NODES = 32
HD = 256
ED = 512
F = 1024
MT = 8
NH = 512
EPS = 1e-5
FLOPS = 2 * 1024 * 1024 * 1024


def regroup(nc, eng, dst, src, one=1.0, cols=slice(0, NH)):
    dv = dst[:, cols, :].rearrange("p (c i) t -> p c t i", i=4)
    sv = src[:, :, cols].rearrange("p t (c i) -> p c t i", i=4)
    if eng == "v":
        nc.vector.tensor_copy(out=dv, in_=sv)
    elif eng == "s":
        nc.scalar.copy(out=dv, in_=sv)
    else:
        nc.gpsimd.tensor_scalar(out=dv, in0=sv, scalar1=one, scalar2=0.0, op0=ALU.mult, op1=ALU.add)


def tile_edgeupdaterwrapper_v01_pa_kernel(tc, p, x_down, ln_edge_g, ln_edge_b, W1, b1, out):
    nc = tc.nc
    p_v = p.rearrange("b i (a m) k -> (b i a) m k", m=MT)
    out_v = out.rearrange("b i (a m) f -> (b i a) m f", m=MT)

    with ExitStack() as ctx:
        const = ctx.enter_context(tc.tile_pool(name="const", bufs=1))
        ps_a = ctx.enter_context(tc.psum_pool(name="ps_a", bufs=4))
        ps_b = ctx.enter_context(tc.psum_pool(name="ps_b", bufs=4))
        ctx.enter_context(tc.manual_schedule())

        p_sb = const.tile([P, MT, ED], BF16, name="p_sb")
        wraw = {}
        wg = {}
        for c in range(2):
            for n in range(2):
                wraw[(c, n)] = const.tile([P, 4, NH], BF16, name="wraw%d%d" % (c, n))
                wg[(c, n)] = const.tile([P, NH, 4], BF16, name="wg%d%d" % (c, n), align_bytes=64)
        token = const.tile([P, 1], F32, name="token")
        eps_t = const.tile([P, 1], F32, name="eps_t")
        junk = const.tile([P, 1], F32, name="junk")
        xx = const.tile([P, 3 * HD], BF16, name="xx")
        su = const.tile([P, P], BF16, name="su")
        bias_bf = const.tile([P, F], BF16, name="bias_bf")
        ident_f = const.tile([P, P], F32, name="ident_f")
        ident_b = const.tile([P, P], BF16, name="ident_b")
        sel_i = const.tile([P, P], BF16, name="sel_i")
        sel_j = const.tile([P, P], BF16, name="sel_j")
        xs = const.tile([P, P], U8, name="xs", align_bytes=64)
        xc = const.tile([P, P], U32, name="xc", align_bytes=64)
        xg = const.tile([P, P, 4], BF16, name="xg", align_bytes=64)
        gb = const.tile([P, 8], F32, name="gb")
        c0 = const.tile([P, MT * P], U32, name="c0", align_bytes=64)
        s0 = const.tile([P, MT * P], U8, name="s0", align_bytes=64)
        stats = const.tile([P, MT, 6], F32, name="stats")
        mv = const.tile([P, MT, 2], F32, name="mv")
        ssq = const.tile([P, MT], F32, name="ssq")
        rstd = const.tile([P, MT], F32, name="rstd")
        nmr = const.tile([P, MT], F32, name="nmr")
        zc = const.tile([P, MT * P], U32, name="zc", align_bytes=64)
        zs = const.tile([P, MT * P], U8, name="zs", align_bytes=64)
        wc = [const.tile([P, F], U32, name="wc%d" % c, align_bytes=64) for c in range(2)]
        ws = [const.tile([P, F], U8, name="ws%d" % c, align_bytes=64) for c in range(2)]
        xn = [const.tile([P, ED], F32, name="xn%d" % m) for m in range(MT)]
        zp = [const.tile([P, 4, NH], BF16, name="zp%d" % g) for g in range(2)]
        zg = [const.tile([P, NH, 4], BF16, name="zg%d" % g, align_bytes=64) for g in range(2)]
        o_sb = [const.tile([P, F], F32, name="o%d" % m) for m in range(MT)]

        nc.vector.memset(su[:], 0.0)
        nc.vector.memset(xx[:], 0.0)
        nc.vector.memset(eps_t[:], EPS)
        nc.vector.memset(xs[:].bitcast(I32), 0)
        make_identity(nc, ident_f[:])
        nc.scalar.activation(out=junk[:], in_=eps_t[:], func=ACT.Abs_reciprocal_sqrt)

        def load_w(c, n):
            cols = slice(n * NH, (n + 1) * NH)
            if c == 0:
                src = W1[0:512, cols].rearrange("(q j) w -> q j w", j=4)
            else:
                src = W1[512:1024, cols].rearrange("(t q) w -> q t w", q=P)
            nc.sync.dma_start(out=wraw[(c, n)][:], in_=src)

        def load_p(a, b):
            nc.sync.dma_start(out=p_sb[:, a:b, :], in_=p_v[:, a:b, :])

        load_p(0, 1)
        load_p(1, 2)
        nc.sync.dma_start(out=xx[0:NODES, HD : 2 * HD], in_=x_down.rearrange("b n k -> (b n) k"))
        load_p(2, 3)
        load_w(0, 0)
        load_p(3, 4)
        load_p(4, 6)
        nc.sync.dma_start(out=su[0:4, :], in_=ln_edge_g.rearrange("(t q) -> t q", q=P))
        nc.sync.dma_start(out=su[4:8, :], in_=ln_edge_b.rearrange("(t q) -> t q", q=P))
        load_w(1, 0)
        load_p(6, 8)
        load_w(1, 1)
        load_w(0, 1)
        nc.sync.dma_start(out=bias_bf[:], in_=b1.partition_broadcast(P))

        nc.vector.tensor_copy(out=ident_b[:], in_=ident_f[:])
        nc.vector.tensor_copy(
            out=sel_i[:].rearrange("p (i a) -> p i a", a=4),
            in_=ident_b[:, 0:NODES].unsqueeze(2).to_broadcast([P, NODES, 4]),
        )
        nc.vector.tensor_copy(
            out=sel_j[:].rearrange("p (m r a) -> p m r a", r=4, a=4),
            in_=ident_b[:, 0:NODES].rearrange("p (a m) -> p m a", a=4).unsqueeze(2).to_broadcast([P, MT, 4, 4]),
        )

        xp = ps_b.tile([P, 4, P], F32, name="xp", tag="b")
        for t in range(4):
            nc.tensor.matmul(xp[:, t, :], lhsT=xx[:, HD + t : 3 * HD : 4], rhs=sel_i[:], start=True, stop=False)
            nc.tensor.matmul(xp[:, t, :], lhsT=xx[:, t : 2 * HD : 4], rhs=sel_j[:], start=False, stop=True)
        su_ps = ps_b.tile([P, P], BF16, name="su_ps", tag="b")
        nc.tensor.transpose(su_ps[:], su[:], ident_b[:])

        def g_copy():
            nc.scalar.copy(out=gb[:], in_=su_ps[:, 0:8])

        def x_copy():
            nc.scalar.copy(out=xg[:], in_=xp[:].rearrange("p t c -> p c t"))

        def x_words():
            nc.vector.quantize_mx(out=xc[:].bitcast(FP8X4), scales=xs[:], in_=xg[:].rearrange("p c t -> p (c t)"))
            xc_i = xc[:].bitcast(I32)
            xs_i = xs[:].bitcast(I32)
            c0_i = c0[:].bitcast(I32)
            s0_i = s0[:].bitcast(I32)
            H = 64
            nc.sync.dma_start(
                out=c0_i[0:H, :].rearrange("p (m c) -> p m c", m=MT),
                in_=xc_i[0:H, :].unsqueeze(1).to_broadcast([H, MT, P]),
            )
            nc.sync.dma_start(
                out=s0_i[0:H, :].rearrange("p (m c) -> p m c", m=MT),
                in_=xs_i[0:H, :].unsqueeze(1).to_broadcast([H, MT, 32]),
            )
            for m in range(MT):
                nc.sync.dma_start(
                    out=c0_i[H:P, m * P : (m + 1) * P].rearrange("p (r c) -> p r c", r=8),
                    in_=xc_i[H:P, m * 16 : (m + 1) * 16].unsqueeze(1).to_broadcast([H, 8, 16]),
                )

        def x_scales():
            H = 64
            xs_i = xs[:].bitcast(I32)
            s0_i = s0[:].bitcast(I32)
            nc.vector.tensor_copy(
                out=s0_i[H:P, :].rearrange("p (m r a) -> p m r a", m=MT, a=4),
                in_=xs_i[H:P, :].rearrange("p (m a) -> p m a", m=MT).unsqueeze(2).to_broadcast([H, MT, 8, 4]),
            )

        def bs(m):
            nc.vector.bn_stats(out=stats[:, m, :], in_=p_sb[:, m, :])

        def ba(m):
            nc.vector.bn_aggr(out=mv[:, m, :], in_=stats[:, m, :])

        def stat_s(m):
            nc.scalar.activation(
                out=xn[m][:], in_=p_sb[:, m, :], func=ACT.Identity, scale=1.0 / ED, accum_out=mv[:, m, 0:1]
            )
            nc.scalar.activation(
                out=xn[m][:], in_=p_sb[:, m, :], func=ACT.Square, scale=-1.0, bias=mv[:, m, 0:1], accum_out=ssq[:, m : m + 1]
            )
            nc.scalar.activation(out=mv[:, m, 1:2], in_=ssq[:, m : m + 1], func=ACT.Identity, scale=1.0 / ED)

        def shift1(m):
            nc.vector.tensor_scalar(
                out=nmr[:, m : m + 1], in0=mv[:, m, 0:1], scalar1=rstd[:, m : m + 1], scalar2=-1.0,
                op0=ALU.mult, op1=ALU.mult,
            )

        def ln_rstd(g):
            ms = slice(4 * g, 4 * g + 4)
            nc.scalar.activation(out=rstd[:, ms], in_=mv[:, ms, 1], func=ACT.Abs_reciprocal_sqrt, bias=eps_t[:, 0:1])

        def ln_shift(g):
            ms = slice(4 * g, 4 * g + 4)
            nc.vector.scalar_tensor_tensor(
                out=nmr[:, ms], in0=mv[:, ms, 0], scalar=-1.0, in1=rstd[:, ms], op0=ALU.mult, op1=ALU.mult
            )

        tps = {}

        def tp_banks(g):
            for t in range(4):
                if g == 0:
                    tps[(g, t)] = ps_a.tile([P, 4, P], F32, name="tpa", tag="a")
                else:
                    tps[(g, t)] = ps_b.tile([P, 4, P], F32, name="tpb", tag="b")

        def ln_norm(m, eng):
            g = m // 4
            if eng == "s":
                nc.scalar.activation(
                    out=xn[m][:], in_=p_sb[:, m, :], func=ACT.Identity, scale=rstd[:, m : m + 1], bias=nmr[:, m : m + 1]
                )
            elif eng == "v":
                nc.vector.tensor_scalar(
                    out=xn[m][:], in0=p_sb[:, m, :], scalar1=mv[:, m, 0:1], scalar2=rstd[:, m : m + 1],
                    op0=ALU.subtract, op1=ALU.mult,
                )
            else:
                nc.gpsimd.tensor_scalar(
                    out=xn[m][:], in0=p_sb[:, m, :], scalar1=rstd[:, m : m + 1], scalar2=nmr[:, m : m + 1],
                    op0=ALU.mult, op1=ALU.add,
                )

        def ln_turn(m):
            for t in range(4):
                nc.tensor.transpose(tps[(m // 4, t)][:, m % 4, :], xn[m][:, t * P : (t + 1) * P], ident_f[:])

        def gain_v(g, t):
            nc.vector.tensor_scalar(
                out=zp[g][:, t, :], in0=tps[(g, t)][:].rearrange("p m c -> p (m c)"),
                scalar1=gb[:, t : t + 1], scalar2=gb[:, 4 + t : 5 + t], op0=ALU.mult, op1=ALU.add,
            )

        def ln_gain(g, ts=range(4)):
            for t in ts:
                nc.scalar.activation(
                    out=zp[g][:, t, :], in_=tps[(g, t)][:].rearrange("p m c -> p (m c)"), func=ACT.Identity,
                    scale=gb[:, t : t + 1], bias=gb[:, 4 + t : 5 + t],
                )

        def z_regroup(g, eng, cols=slice(0, NH)):
            regroup(nc, eng, zg[g][:], zp[g][:], 1.0, cols)

        def z_quant(g):
            cols = slice(g * NH, (g + 1) * NH)
            nc.vector.quantize_mx(
                out=zc[:, cols].bitcast(FP8X4), scales=zs[:, cols], in_=zg[g][:].rearrange("p w t -> p (w t)")
            )

        def w_regroup(c, n, eng, one=1.0, cols=slice(0, NH)):
            regroup(nc, eng, wg[(c, n)][:], wraw[(c, n)][:], one, cols)

        def w_quant(c, n):
            cols = slice(n * NH, (n + 1) * NH)
            nc.vector.quantize_mx(
                out=wc[c][:, cols].bitcast(FP8X4), scales=ws[c][:, cols], in_=wg[(c, n)][:].rearrange("p w t -> p (w t)")
            )

        def warm(k, dst):
            for rep in range(k):
                nc.tensor.matmul(dst, lhsT=ident_f[:], rhs=ident_f[:], start=True, stop=True)

        accs = {}

        def acc_bank(m, n):
            if m < 4 or n == 1:
                accs[(m, n)] = ps_a.tile([P, NH], F32, name="acc", tag="a")
            else:
                accs[(m, n)] = ps_b.tile([P, NH], F32, name="acc", tag="b")

        def mm(m, n):
            rows = slice(m * P, (m + 1) * P)
            cols = slice(n * NH, (n + 1) * NH)
            acc = accs[(m, n)]
            nc.tensor.matmul_mx(
                out=acc[:], lhsT=c0[:, rows].bitcast(FP8X4), lhsT_scale=s0[:, rows],
                rhs=wc[0][:, cols].bitcast(FP8X4), rhs_scale=ws[0][:, cols], start=True, stop=False,
            )
            nc.tensor.matmul_mx(
                out=acc[:], lhsT=zc[:, rows].bitcast(FP8X4), lhsT_scale=zs[:, rows],
                rhs=wc[1][:, cols].bitcast(FP8X4), rhs_scale=ws[1][:, cols], start=False, stop=True,
            )

        def add_bias(m, n, a=0, b=NH):
            cols = slice(n * NH + a, n * NH + b)
            nc.vector.tensor_tensor(out=o_sb[m][:, cols], in0=accs[(m, n)][:, a:b], in1=bias_bf[:, cols], op=ALU.add)

        def add_bias_g(m, n):
            cols = slice(n * NH, (n + 1) * NH)
            nc.scalar.copy(out=o_sb[m][:, cols], in_=accs[(m, n)][:])
            nc.gpsimd.tensor_tensor(out=o_sb[m][:, cols], in0=o_sb[m][:, cols], in1=bias_bf[:, cols], op=ALU.add)

        def finish(m, n, eng, a=0, b=NH):
            cols = slice(n * NH + a, n * NH + b)
            if eng == "s":
                nc.scalar.activation(out=o_sb[m][:, cols], in_=o_sb[m][:, cols], func=ACT.Relu)
            elif eng == "v":
                nc.vector.tensor_scalar_max(out=o_sb[m][:, cols], in0=o_sb[m][:, cols], scalar1=0.0)
            else:
                nc.gpsimd.tensor_scalar(
                    out=o_sb[m][:, cols], in0=o_sb[m][:, cols], scalar1=float("inf"), scalar2=0.0, op0=ALU.min, op1=ALU.max
                )
            nc.sync.dma_start(out=out_v[:, m, cols], in_=o_sb[m][:, cols])

        A = range(0, 4)
        B = range(4, 8)
        lo, hi = slice(0, NH // 2), slice(NH // 2, NH)
        w_regroup(0, 0, "g")
        bs(0)
        stat_s(1)
        x_copy()
        bs(2)
        ba(0)
        ba(2)
        bs(3)
        ba(3)
        ln_rstd(0)
        g_copy()
        w_regroup(1, 0, "s")
        bs(4)
        bs(5)
        ba(4)
        ba(5)
        tp_banks(0)
        warm(3, tps[(0, 3)][:, 3, :])
        for m in A:
            ln_norm(m, "v")
            ln_turn(m)
        nc.vector.memset(token[:], 1.0)
        w_regroup(1, 1, "g", token[:, 0:1], lo)
        bs(6)
        bs(7)
        ba(6)
        ba(7)
        ln_gain(0, (0, 1))
        ln_rstd(1)
        ln_gain(0, (2,))
        x_words()
        w_quant(0, 0)
        ln_shift(1)
        x_scales()
        gain_v(0, 3)
        tp_banks(1)
        for m in B:
            ln_norm(m, "s")
            ln_turn(m)
        z_regroup(0, "v")
        w_quant(1, 0)
        z_quant(0)
        w_regroup(1, 1, "s", 1.0, hi)
        for m in A:
            acc_bank(m, 0)
        for m in A:
            mm(m, 0)
        ln_gain(1)
        w_regroup(0, 1, "v")
        w_quant(1, 1)
        w_quant(0, 1)
        z_regroup(1, "g", lo)
        z_regroup(1, "s", hi)
        for m in A:
            add_bias(m, 0)
            finish(m, 0, "ssss"[m])
        for m in A:
            acc_bank(m, 1)
            mm(m, 1)
        z_quant(1)
        for m in A:
            add_bias(m, 1)
            finish(m, 1, "gsgs"[m])
        for n in range(2):
            for m in B:
                acc_bank(m, n)
                mm(m, n)
            for m in B:
                if (m, n) == (7, 1):
                    add_bias(m, n, 0, NH // 2)
                    finish(m, n, "s", 0, NH // 2)
                    add_bias(m, n, NH // 2, NH)
                    finish(m, n, "s", NH // 2, NH)
                else:
                    add_bias(m, n)
                    finish(m, n, ("sgss", "gssss")[n][m - 4])
